import numpy as np
import ml_dtypes


def mxq(x, axis, fmt="e4m3"):
    dtype, down = {"e4m3": (ml_dtypes.float8_e4m3fn, 7), "e5m2": (ml_dtypes.float8_e5m2, 14)}[fmt]
    v = np.moveaxis(np.asarray(x, np.float32).astype(ml_dtypes.bfloat16).astype(np.float64), axis, -1)
    blocks = v.reshape(v.shape[:-1] + (-1, 32))
    amax = np.abs(blocks).max(-1, keepdims=True)
    byte = np.maximum(np.where(amax > 0, np.frexp(amax)[1] - 1 + 127, 0) - down, 1)
    scale = np.exp2(byte - 127.0)
    codes = (blocks / scale).astype(np.float32).astype(dtype).astype(np.float64)
    return np.moveaxis((codes * scale).reshape(v.shape), -1, axis)


BF16 = ml_dtypes.bfloat16


def bf(x):
    return np.asarray(x, np.float32).astype(BF16)


def f64(x):
    return np.asarray(x).astype(np.float64)


P, R, C = 512, 512, 1536


def softmax_rows(v):
    e = np.exp(v - v.max(-1, keepdims=True))
    return e / e.sum(-1, keepdims=True)


def setup_inputs():
    return {"initial_facts": bf(np.random.uniform(0.0, 1.0, (P, C))),
            "rule_weights": bf(np.random.standard_normal((R, P)) * 1.5)}


def reference(initial_facts, rule_weights):
    a = mxq(softmax_rows(f64(rule_weights)), 1, "e4m3")
    facts = f64(initial_facts)
    derived = a @ mxq(facts, 0, "e4m3")
    facts = np.maximum(facts, derived.max(axis=0))
    derived = a @ mxq(facts, 0, "e4m3")
    return np.maximum(facts, derived.max(axis=0))

@@ -1,0 +1,213 @@
+from contextlib import ExitStack
+
+import concourse.mybir as mybir
+from concourse.masks import make_identity
+
+FP8X4 = mybir.dt.float8_e4m3fn_x4
+BF16 = mybir.dt.bfloat16
+F32 = mybir.dt.float32
+U32 = mybir.dt.uint32
+U8 = mybir.dt.uint8
+MAX = mybir.AluOpType.max
+MULT = mybir.AluOpType.mult
+AX = mybir.AxisListType.X
+EXP = mybir.ActivationFunctionType.Exp
+
+P = 128
+T = 4
+R = 512
+C = 1536
+CH = 512
+NCH = C // CH
+BPC = CH // P
+NB = C // P
+
+FLOPS = 2 * 2 * 512 * 512 * 1536
+
+
+def tile_differentiableilp_pa_kernel(tc, initial_facts, rule_weights, out):
+    nc = tc.nc
+    facts_v = initial_facts.rearrange("(t q) c -> q t c", q=P)
+    out_v = out.rearrange("(t q) c -> q t c", q=P)
+
+    with ExitStack() as ctx:
+        sb = ctx.enter_context(tc.tile_pool(name="sb", bufs=1))
+        ps_mx = ctx.enter_context(tc.psum_pool(name="psmx", bufs=4))
+        ps_aux = ctx.enter_context(tc.psum_pool(name="psaux", bufs=4))
+        ctx.enter_context(tc.manual_schedule())
+
+        w_sb = [sb.tile([P, R], BF16, name="w_sb%d" % b) for b in range(4)]
+        f_sb = [sb.tile([P, T, CH], BF16, name="f_sb%d" % k) for k in range(NCH)]
+        ident_bf = sb.tile([P, P], BF16, name="ident_bf")
+        ident_f = sb.tile([P, P], F32, name="ident_f")
+        dup = sb.tile([P, P, 2], BF16, name="dup")
+        nmax = sb.tile([P, 4], F32, name="nmax")
+        ssum = sb.tile([P, 4], F32, name="ssum")
+        rsum = sb.tile([P, 4], F32, name="rsum")
+        e_sb = [sb.tile([P, R], F32, name="e_sb%d" % b) for b in range(4)]
+        a_bf = [sb.tile([P, R], BF16, name="a_bf%d" % b) for b in range(4)]
+        a_g = sb.tile([P, R, T], BF16, name="a_g", align_bytes=64)
+        a_q = sb.tile([P, R], U32, name="a_q", align_bytes=64)
+        a_s = sb.tile([P, R], U8, name="a_s", align_bytes=64)
+        f_g = [sb.tile([P, CH, T], BF16, name="f_g%d" % k, align_bytes=64) for k in range(NCH)]
+        f_q = [sb.tile([P, CH], U32, name="f_q%d" % k, align_bytes=64) for k in range(NCH)]
+        f_s = [sb.tile([P, CH], U8, name="f_s%d" % k, align_bytes=64) for k in range(NCH)]
+        g_g = [sb.tile([P, CH, T], BF16, name="g_g%d" % k, align_bytes=64) for k in range(NCH)]
+        g_q = [sb.tile([P, CH], U32, name="g_q%d" % k, align_bytes=64) for k in range(NCH)]
+        g_s = [sb.tile([P, CH], U8, name="g_s%d" % k, align_bytes=64) for k in range(NCH)]
+        m1 = [sb.tile([P, BPC], F32, name="m1_%d" % k) for k in range(NCH)]
+        m1b = [sb.tile([P, BPC], BF16, name="m1b_%d" % k) for k in range(NCH)]
+        m2 = [sb.tile([P, BPC], F32, name="m2_%d" % k) for k in range(NCH)]
+        mm = [sb.tile([P, BPC], F32, name="mm_%d" % k) for k in range(NCH)]
+        o_sb = [sb.tile([P, T, CH], F32, name="o_sb%d" % k) for k in range(NCH)]
+
+        for b in range(4):
+            nc.sync.dma_start(out=w_sb[b][:], in_=rule_weights[b * P:(b + 1) * P, :])
+        for k in range(NCH):
+            nc.sync.dma_start(out=f_sb[k][:], in_=facts_v[:, :, k * CH:(k + 1) * CH])
+
+        make_identity(nc, ident_bf[:])
+        make_identity(nc, ident_f[:])
+        nc.gpsimd.tensor_copy(out=dup[:], in_=ident_bf[:].unsqueeze(2).to_broadcast([P, P, 2]))
+
+        def regroup(engine_copy, k):
+            engine_copy(
+                out=f_g[k][:].rearrange("p (c i) t -> p c t i", i=4),
+                in_=f_sb[k][:].rearrange("p t (c i) -> p c t i", i=4),
+            )
+
+        def quant(g, q, s):
+            nc.vector.quantize_mx(
+                out=q[:].bitcast(FP8X4), scales=s[:], in_=g[:].rearrange("p c t -> p (c t)")
+            )
+
+        acc = {}
+
+        def mx(step, j):
+            k, jj = divmod(j, BPC)
+            q, s = (f_q[k], f_s[k]) if step == 1 else (g_q[k], g_s[k])
+            a = ps_mx.tile([P, R], F32, name="acc%d_%d" % (step, j), tag="acc")
+            nc.tensor.matmul_mx(
+                out=a[:],
+                lhsT=q[:, jj * P:(jj + 1) * P].bitcast(FP8X4),
+                lhsT_scale=s[:, jj * P:(jj + 1) * P],
+                rhs=a_q[:].bitcast(FP8X4),
+                rhs_scale=a_s[:],
+                start=True,
+                stop=True,
+            )
+            acc[(step, j)] = a
+
+        def red(step, j):
+            k, jj = divmod(j, BPC)
+            m = m1[k] if step == 1 else m2[k]
+            nc.vector.tensor_reduce(out=m[:, jj:jj + 1], in_=acc[(step, j)][:], axis=AX, op=MAX)
+
+        pb1 = {}
+        pb2 = {}
+
+        def spread1(k):
+            nc.vector.tensor_copy(out=m1b[k][:], in_=m1[k][:])
+            pb = ps_aux.tile([P, CH, 2], BF16, name="pb1_%d" % k, tag="aux")
+            for jj in range(BPC):
+                nc.tensor.matmul(
+                    out=pb[:, jj * P:(jj + 1) * P, :].rearrange("p c e -> p (c e)"),
+                    lhsT=m1b[k][:, jj:jj + 1].to_broadcast([P, P]),
+                    rhs=dup[:].rearrange("p c e -> p (c e)"),
+                    start=True,
+                    stop=True,
+                )
+            pb1[k] = pb
+
+        def facts1(k):
+            nc.vector.tensor_tensor(
+                out=g_g[k][:].rearrange("p c (u e) -> p c u e", e=2),
+                in0=f_g[k][:].rearrange("p c (u e) -> p c u e", e=2),
+                in1=pb1[k][:].unsqueeze(2).to_broadcast([P, CH, 2, 2]),
+                op=MAX,
+            )
+
+        def spread2(k):
+            nc.vector.tensor_tensor(out=mm[k][:], in0=m1[k][:], in1=m2[k][:], op=MAX)
+            pb = ps_aux.tile([P, CH], F32, name="pb2_%d" % k, tag="aux")
+            for jj in range(BPC):
+                nc.tensor.transpose(
+                    out=pb[:, jj * P:(jj + 1) * P],
+                    in_=mm[k][:, jj:jj + 1].to_broadcast([P, P]),
+                    identity=ident_f[:],
+                )
+            pb2[k] = pb
+
+        def final(k, t0, t1):
+            nc.vector.tensor_tensor(
+                out=o_sb[k][:, t0:t1, :],
+                in0=f_sb[k][:, t0:t1, :],
+                in1=pb2[k][:].unsqueeze(1).to_broadcast([P, t1 - t0, CH]),
+                op=MAX,
+            )
+            nc.sync.dma_start(out=out_v[:, t0:t1, k * CH:(k + 1) * CH], in_=o_sb[k][:, t0:t1, :])
+
+        for b in range(4):
+            nc.vector.tensor_reduce(out=nmax[:, b:b + 1], in_=w_sb[b][:], axis=AX, op=MAX, negate=True)
+            nc.scalar.activation(
+                out=e_sb[b][:], in_=w_sb[b][:], func=EXP, bias=nmax[:, b:b + 1], scale=1.0,
+                accum_out=ssum[:, b:b + 1],
+            )
+        for b in range(4):
+            nc.vector.reciprocal(out=rsum[:, b:b + 1], in_=ssum[:, b:b + 1])
+            nc.vector.tensor_scalar(
+                out=a_bf[b][:], in0=e_sb[b][:], scalar1=rsum[:, b:b + 1], scalar2=None, op0=MULT
+            )
+            pa = ps_aux.tile([P, T, P], BF16, name="pa%d" % b, tag="aux")
+            for t in range(T):
+                nc.tensor.transpose(out=pa[:, t, :], in_=a_bf[b][:, t * P:(t + 1) * P], identity=ident_bf[:])
+            nc.scalar.copy(out=a_g[:, b * P:(b + 1) * P, :], in_=pa[:].rearrange("q t r -> q r t"))
+        regroup(nc.vector.tensor_copy, 0)
+        regroup(nc.scalar.copy, 1)
+        regroup(nc.scalar.copy, 2)
+        quant(f_g[0], f_q[0], f_s[0])
+        quant(a_g, a_q, a_s)
+
+        for j in range(4):
+            mx(1, j)
+        quant(f_g[1], f_q[1], f_s[1])
+        for j in range(4):
+            red(1, j)
+            mx(1, j + 4)
+        spread1(0)
+        quant(f_g[2], f_q[2], f_s[2])
+        for j in range(4, 8):
+            red(1, j)
+            mx(1, j + 4)
+        spread1(1)
+        facts1(0)
+        red(1, 8)
+        quant(g_g[0], g_q[0], g_s[0])
+        mx(2, 0)
+        for j in range(9, 12):
+            red(1, j)
+            mx(2, j - 8)
+        spread1(2)
+        facts1(1)
+        red(2, 0)
+        quant(g_g[1], g_q[1], g_s[1])
+        mx(2, 4)
+        for j in range(1, 4):
+            red(2, j)
+            mx(2, j + 4)
+        spread2(0)
+        facts1(2)
+        red(2, 4)
+        quant(g_g[2], g_q[2], g_s[2])
+        mx(2, 8)
+        for j in range(5, 8):
+            red(2, j)
+            mx(2, j + 4)
+        spread2(1)
+        final(0, 0, T)
+        for j in range(8, 12):
+            red(2, j)
+        spread2(2)
+        final(1, 0, T)
+        for t in range(T):
+            final(2, t, t + 1)

@@ -9,7 +9,9 @@ F32 = mybir.dt.float32
 U32 = mybir.dt.uint32
 U8 = mybir.dt.uint8
 MAX = mybir.AluOpType.max
+MIN = mybir.AluOpType.min
 MULT = mybir.AluOpType.mult
+ADD = mybir.AluOpType.add
 AX = mybir.AxisListType.X
 EXP = mybir.ActivationFunctionType.Exp
 
@@ -19,10 +21,22 @@ R = 512
 C = 1536
 CH = 512
 NCH = C // CH
-BPC = CH // P
-NB = C // P
+GW = 256
+NG = C // GW
+BPG = GW // P
+GPC = CH // GW
+BIG = 3.0e38
 
 FLOPS = 2 * 2 * 512 * 512 * 1536
+
+FINAL_MODE = ["G", "G", "G", "G", "D", "D"]
+RG_ENGINE = ["G", "G", "S", "S", "S", "S"]
+EXIT_ENGINE = ["S", "S", "S", "V"]
+ACC_BUFS = 4
+CV_ENGINE = "V"
+RIPE = [2, 3]
+FLIP_AT = 0
+ROWMAX_2X = True
 
 
 def tile_differentiableilp_pa_kernel(tc, initial_facts, rule_weights, out):
@@ -32,61 +46,84 @@ def tile_differentiableilp_pa_kernel(tc, initial_facts, rule_weights, out):
 
     with ExitStack() as ctx:
         sb = ctx.enter_context(tc.tile_pool(name="sb", bufs=1))
-        ps_mx = ctx.enter_context(tc.psum_pool(name="psmx", bufs=4))
-        ps_aux = ctx.enter_context(tc.psum_pool(name="psaux", bufs=4))
+        rot = ctx.enter_context(tc.tile_pool(name="rot", bufs=4))
+        ps_acc = ctx.enter_context(tc.psum_pool(name="psacc", bufs=ACC_BUFS))
+        ps_b1 = ctx.enter_context(tc.psum_pool(name="psb1", bufs=1))
+        ps_tr = ctx.enter_context(tc.psum_pool(name="pstr", bufs=1))
+        ps_o = ctx.enter_context(tc.psum_pool(name="pso", bufs=2))
         ctx.enter_context(tc.manual_schedule())
 
         w_sb = [sb.tile([P, R], BF16, name="w_sb%d" % b) for b in range(4)]
-        f_sb = [sb.tile([P, T, CH], BF16, name="f_sb%d" % k) for k in range(NCH)]
+        f_first = [sb.tile([P, T, GW], BF16, name="f_first%d" % h) for h in range(GPC)]
+        f_sb = [sb.tile([P, T, CH], BF16, name="f_sb%d" % k) for k in range(1, NCH)]
         ident_bf = sb.tile([P, P], BF16, name="ident_bf")
         ident_f = sb.tile([P, P], F32, name="ident_f")
         dup = sb.tile([P, P, 2], BF16, name="dup")
+        w_neg = sb.tile([P, R], BF16, name="w_neg")
+        warm = sb.tile([P, 2], F32, name="warm")
         nmax = sb.tile([P, 4], F32, name="nmax")
         ssum = sb.tile([P, 4], F32, name="ssum")
         rsum = sb.tile([P, 4], F32, name="rsum")
         e_sb = [sb.tile([P, R], F32, name="e_sb%d" % b) for b in range(4)]
         a_bf = [sb.tile([P, R], BF16, name="a_bf%d" % b) for b in range(4)]
-        a_g = sb.tile([P, R, T], BF16, name="a_g", align_bytes=64)
+        a_g = [sb.tile([P, P, T], BF16, name="a_g%d" % b, align_bytes=64) for b in range(4)]
         a_q = sb.tile([P, R], U32, name="a_q", align_bytes=64)
         a_s = sb.tile([P, R], U8, name="a_s", align_bytes=64)
-        f_g = [sb.tile([P, CH, T], BF16, name="f_g%d" % k, align_bytes=64) for k in range(NCH)]
-        f_q = [sb.tile([P, CH], U32, name="f_q%d" % k, align_bytes=64) for k in range(NCH)]
-        f_s = [sb.tile([P, CH], U8, name="f_s%d" % k, align_bytes=64) for k in range(NCH)]
-        g_g = [sb.tile([P, CH, T], BF16, name="g_g%d" % k, align_bytes=64) for k in range(NCH)]
-        g_q = [sb.tile([P, CH], U32, name="g_q%d" % k, align_bytes=64) for k in range(NCH)]
-        g_s = [sb.tile([P, CH], U8, name="g_s%d" % k, align_bytes=64) for k in range(NCH)]
-        m1 = [sb.tile([P, BPC], F32, name="m1_%d" % k) for k in range(NCH)]
-        m1b = [sb.tile([P, BPC], BF16, name="m1b_%d" % k) for k in range(NCH)]
-        m2 = [sb.tile([P, BPC], F32, name="m2_%d" % k) for k in range(NCH)]
-        mm = [sb.tile([P, BPC], F32, name="mm_%d" % k) for k in range(NCH)]
-        o_sb = [sb.tile([P, T, CH], F32, name="o_sb%d" % k) for k in range(NCH)]
+        f_g = [sb.tile([P, GW, T], BF16, name="f_g%d" % g, align_bytes=64) for g in range(NG)]
+        f_q = [sb.tile([P, GW], U32, name="f_q%d" % g, align_bytes=64) for g in range(NG)]
+        f_s = [sb.tile([P, GW], U8, name="f_s%d" % g, align_bytes=64) for g in range(NG)]
+        g_g = [sb.tile([P, GW, T], BF16, name="g_g%d" % g, align_bytes=64) for g in range(NG)]
+        g_q = [sb.tile([P, GW], U32, name="g_q%d" % g, align_bytes=64) for g in range(NG)]
+        g_s = [sb.tile([P, GW], U8, name="g_s%d" % g, align_bytes=64) for g in range(NG)]
+        m1 = [sb.tile([P, BPG], F32, name="m1_%d" % g) for g in range(NG)]
+        m1b = [sb.tile([P, BPG], BF16, name="m1b_%d" % g) for g in range(NG)]
+        m2 = [sb.tile([P, BPG], F32, name="m2_%d" % g) for g in range(NG)]
+        mm = [sb.tile([P, BPG], F32, name="mm_%d" % g) for g in range(NG)]
+        f_t = [sb.tile([P, BPG, R], BF16, name="f_t%d" % g) for g in range(NG)]
+        o_sb = [sb.tile([P, T, GW], F32, name="o_sb%d" % g) for g in range(NG)]
+
+        def fsl(g):
+            k, h = divmod(g, GPC)
+            if k == 0:
+                return f_first[h][:]
+            return f_sb[k - 1][:, :, h * GW:(h + 1) * GW]
 
         for b in range(4):
             nc.sync.dma_start(out=w_sb[b][:], in_=rule_weights[b * P:(b + 1) * P, :])
-        for k in range(NCH):
-            nc.sync.dma_start(out=f_sb[k][:], in_=facts_v[:, :, k * CH:(k + 1) * CH])
+        for h in range(GPC):
+            nc.sync.dma_start(out=f_first[h][:], in_=facts_v[:, :, h * GW:(h + 1) * GW])
+        for k in range(1, NCH):
+            nc.sync.dma_start(out=f_sb[k - 1][:], in_=facts_v[:, :, k * CH:(k + 1) * CH])
 
+        nc.vector.memset(warm[:], 0.0)
+        nc.scalar.activation(out=warm[:, 1:2], in_=warm[:, 0:1], func=EXP)
         make_identity(nc, ident_bf[:])
         make_identity(nc, ident_f[:])
         nc.gpsimd.tensor_copy(out=dup[:], in_=ident_bf[:].unsqueeze(2).to_broadcast([P, P, 2]))
 
-        def regroup(engine_copy, k):
-            engine_copy(
-                out=f_g[k][:].rearrange("p (c i) t -> p c t i", i=4),
-                in_=f_sb[k][:].rearrange("p t (c i) -> p c t i", i=4),
-            )
+        def regroup(g):
+            dst = f_g[g][:].rearrange("p (c i) t -> p c t i", i=4)
+            src = fsl(g).rearrange("p t (c i) -> p c t i", i=4)
+            if RG_ENGINE[g] == "G":
+                nc.gpsimd.tensor_scalar(out=dst, in0=src, scalar1=1.0, scalar2=0.0, op0=MULT, op1=ADD)
+            elif RG_ENGINE[g] == "S":
+                nc.scalar.copy(out=dst, in_=src)
+            else:
+                nc.vector.tensor_copy(out=dst, in_=src)
 
-        def quant(g, q, s):
-            nc.vector.quantize_mx(
-                out=q[:].bitcast(FP8X4), scales=s[:], in_=g[:].rearrange("p c t -> p (c t)")
-            )
+        def quant(src, q, s):
+            nc.vector.quantize_mx(out=q.bitcast(FP8X4), scales=s, in_=src.rearrange("p c t -> p (c t)"))
 
         acc = {}
+        quantised = set()
+        order = []
+        state = {"next": 0, "open": 0, "a_ready": 0, "reds": 0}
+        waiting = []
 
         def mx(step, j):
-            k, jj = divmod(j, BPC)
-            q, s = (f_q[k], f_s[k]) if step == 1 else (g_q[k], g_s[k])
-            a = ps_mx.tile([P, R], F32, name="acc%d_%d" % (step, j), tag="acc")
+            g, jj = divmod(j, BPG)
+            q, s = (f_q[g], f_s[g]) if step == 1 else (g_q[g], g_s[g])
+            a = ps_acc.tile([P, R], F32, name="acc%d_%d" % (step, j), tag="acc")
             nc.tensor.matmul_mx(
                 out=a[:],
                 lhsT=q[:, jj * P:(jj + 1) * P].bitcast(FP8X4),
@@ -98,116 +135,219 @@ def tile_differentiableilp_pa_kernel(tc, initial_facts, rule_weights, out):
             )
             acc[(step, j)] = a
 
+        def feed():
+            while state["a_ready"] and state["next"] < len(order) and state["open"] < ACC_BUFS:
+                step, j = order[state["next"]]
+                if (step, j // BPG) not in quantised:
+                    break
+                mx(step, j)
+                state["next"] += 1
+                state["open"] += 1
+
+        def fill():
+            for n in range(len(waiting)):
+                if waiting[n][0] <= state["reds"]:
+                    waiting.pop(n)[1]()
+                    return
+
         def red(step, j):
-            k, jj = divmod(j, BPC)
-            m = m1[k] if step == 1 else m2[k]
+            g, jj = divmod(j, BPG)
+            m = m1[g] if step == 1 else m2[g]
             nc.vector.tensor_reduce(out=m[:, jj:jj + 1], in_=acc[(step, j)][:], axis=AX, op=MAX)
+            state["open"] -= 1
+            state["reds"] += 1
+            feed()
+            fill()
 
         pb1 = {}
-        pb2 = {}
 
-        def spread1(k):
-            nc.vector.tensor_copy(out=m1b[k][:], in_=m1[k][:])
-            pb = ps_aux.tile([P, CH, 2], BF16, name="pb1_%d" % k, tag="aux")
-            for jj in range(BPC):
+        def round1(g):
+            if CV_ENGINE == "S":
+                nc.scalar.copy(out=m1b[g][:], in_=m1[g][:])
+            else:
+                nc.vector.tensor_copy(out=m1b[g][:], in_=m1[g][:])
+
+        def spread1(g):
+            pb = ps_b1.tile([P, GW, 2], BF16, name="pb1_%d" % g, tag="pb1")
+            for jj in range(BPG):
                 nc.tensor.matmul(
                     out=pb[:, jj * P:(jj + 1) * P, :].rearrange("p c e -> p (c e)"),
-                    lhsT=m1b[k][:, jj:jj + 1].to_broadcast([P, P]),
+                    lhsT=m1b[g][:, jj:jj + 1].to_broadcast([P, P]),
                     rhs=dup[:].rearrange("p c e -> p (c e)"),
                     start=True,
                     stop=True,
                 )
-            pb1[k] = pb
+            pb1[g] = pb
 
-        def facts1(k):
+        def facts1(g):
             nc.vector.tensor_tensor(
-                out=g_g[k][:].rearrange("p c (u e) -> p c u e", e=2),
-                in0=f_g[k][:].rearrange("p c (u e) -> p c u e", e=2),
-                in1=pb1[k][:].unsqueeze(2).to_broadcast([P, CH, 2, 2]),
+                out=g_g[g][:].rearrange("p c (u e) -> p c u e", e=2),
+                in0=f_g[g][:].rearrange("p c (u e) -> p c u e", e=2),
+                in1=pb1[g][:].unsqueeze(2).to_broadcast([P, GW, 2, 2]),
                 op=MAX,
             )
 
-        def spread2(k):
-            nc.vector.tensor_tensor(out=mm[k][:], in0=m1[k][:], in1=m2[k][:], op=MAX)
-            pb = ps_aux.tile([P, CH], F32, name="pb2_%d" % k, tag="aux")
-            for jj in range(BPC):
-                nc.tensor.transpose(
-                    out=pb[:, jj * P:(jj + 1) * P],
-                    in_=mm[k][:, jj:jj + 1].to_broadcast([P, P]),
-                    identity=ident_f[:],
+        def quant1(g):
+            quant(g_g[g][:], g_q[g][:], g_s[g][:])
+            quantised.add((2, g))
+            feed()
+
+        def quant0(g):
+            quant(f_g[g][:], f_q[g][:], f_s[g][:])
+            quantised.add((1, g))
+            feed()
+
+        def flip_facts(g):
+            pf = ps_tr.tile([P, BPG, R], BF16, name="pf%d" % g, tag="tr")
+            src = fsl(g)
+            for jj in range(BPG):
+                for t in range(T):
+                    nc.tensor.transpose(
+                        out=pf[:, jj, t * P:(t + 1) * P], in_=src[:, t, jj * P:(jj + 1) * P], identity=ident_bf[:]
+                    )
+            nc.scalar.copy(out=f_t[g][:], in_=pf[:])
+
+        ots = {}
+
+        def final_max(g):
+            mode = FINAL_MODE[g]
+            if mode == "D":
+                nc.vector.tensor_tensor(out=mm[g][:], in0=m1[g][:], in1=m2[g][:], op=MAX)
+                if g % 2 == 0:
+                    pb = ps_tr.tile([P, GW], F32, name="pb2_%d" % g, tag="tr")
+                else:
+                    pb = ps_b1.tile([P, GW], F32, name="pb2_%d" % g, tag="pb1")
+                for jj in range(BPG):
+                    nc.tensor.transpose(
+                        out=pb[:, jj * P:(jj + 1) * P],
+                        in_=mm[g][:, jj:jj + 1].to_broadcast([P, P]),
+                        identity=ident_f[:],
+                    )
+                ots[g] = pb
+                return
+            for jj in range(BPG):
+                ot = rot.tile([P, R], F32, name="ot%d_%d" % (g, jj), tag="ot")
+                if mode == "G":
+                    nc.gpsimd.tensor_scalar(
+                        out=mm[g][:, jj:jj + 1], in0=m2[g][:, jj:jj + 1], scalar1=BIG,
+                        scalar2=m1[g][:, jj:jj + 1], op0=MIN, op1=MAX,
+                    )
+                    nc.gpsimd.tensor_scalar(
+                        out=ot[:], in0=f_t[g][:, jj, :], scalar1=BIG, scalar2=mm[g][:, jj:jj + 1], op0=MIN, op1=MAX
+                    )
+                else:
+                    nc.vector.tensor_scalar(
+                        out=ot[:], in0=f_t[g][:, jj, :], scalar1=m1[g][:, jj:jj + 1],
+                        scalar2=m2[g][:, jj:jj + 1], op0=MAX, op1=MAX,
+                    )
+                ots[(g, jj)] = ot
+
+        def final_direct(g, halves):
+            for t0 in halves:
+                nc.vector.tensor_tensor(
+                    out=o_sb[g][:, t0:t0 + 2, :],
+                    in0=fsl(g)[:, t0:t0 + 2, :],
+                    in1=ots[g][:].unsqueeze(1).to_broadcast([P, 2, GW]),
+                    op=MAX,
                 )
-            pb2[k] = pb
+                nc.sync.dma_start(out=out_v[:, t0:t0 + 2, g * GW:(g + 1) * GW], in_=o_sb[g][:, t0:t0 + 2, :])
 
-        def final(k, t0, t1):
-            nc.vector.tensor_tensor(
-                out=o_sb[k][:, t0:t1, :],
-                in0=f_sb[k][:, t0:t1, :],
-                in1=pb2[k][:].unsqueeze(1).to_broadcast([P, t1 - t0, CH]),
-                op=MAX,
-            )
-            nc.sync.dma_start(out=out_v[:, t0:t1, k * CH:(k + 1) * CH], in_=o_sb[k][:, t0:t1, :])
+        def final_flip(gj):
+            g, jj = gj
+            po = ps_o.tile([P, T, P], F32, name="po%d_%d" % (g, jj), tag="po")
+            for t in range(T):
+                nc.tensor.transpose(out=po[:, t, :], in_=ots[(g, jj)][:, t * P:(t + 1) * P], identity=ident_f[:])
+            nc.scalar.copy(out=o_sb[g][:, :, jj * P:(jj + 1) * P], in_=po[:])
+            if jj == BPG - 1:
+                nc.sync.dma_start(out=out_v[:, :, g * GW:(g + 1) * GW], in_=o_sb[g][:])
+
+        def later(delay, fn, g):
+            waiting.append((state["reds"] + delay, lambda: fn(g)))
+
+        for i in range(NG + 2):
+            if i < NG:
+                order.extend([(1, BPG * i + jj) for jj in range(BPG)])
+            if 0 <= i - 2 < NG:
+                order.extend([(2, BPG * (i - 2) + jj) for jj in range(BPG)])
 
         for b in range(4):
-            nc.vector.tensor_reduce(out=nmax[:, b:b + 1], in_=w_sb[b][:], axis=AX, op=MAX, negate=True)
+            if ROWMAX_2X:
+                nc.vector.tensor_scalar(
+                    out=w_neg[:], in0=w_sb[b][:], scalar1=-1.0, scalar2=None, op0=MULT, op1=MIN,
+                    accum_out=nmax[:, b:b + 1],
+                )
+            else:
+                nc.vector.tensor_reduce(out=nmax[:, b:b + 1], in_=w_sb[b][:], axis=AX, op=MAX, negate=True)
             nc.scalar.activation(
                 out=e_sb[b][:], in_=w_sb[b][:], func=EXP, bias=nmax[:, b:b + 1], scale=1.0,
                 accum_out=ssum[:, b:b + 1],
             )
+        for g in range(NG):
+            if RG_ENGINE[g] == "G":
+                regroup(g)
+        pas = []
+
+        def a_exit(bb):
+            cp = nc.scalar.copy if EXIT_ENGINE[bb] == "S" else nc.vector.tensor_copy
+            cp(out=a_g[bb][:], in_=pas[bb][:].rearrange("q t r -> q r t"))
+
+        def a_quant(bb):
+            quant(a_g[bb][:], a_q[:, bb * P:(bb + 1) * P], a_s[:, bb * P:(bb + 1) * P])
+
         for b in range(4):
             nc.vector.reciprocal(out=rsum[:, b:b + 1], in_=ssum[:, b:b + 1])
             nc.vector.tensor_scalar(
                 out=a_bf[b][:], in0=e_sb[b][:], scalar1=rsum[:, b:b + 1], scalar2=None, op0=MULT
             )
-            pa = ps_aux.tile([P, T, P], BF16, name="pa%d" % b, tag="aux")
+            pa = ps_acc.tile([P, T, P], BF16, name="pa%d" % b, tag="acc")
             for t in range(T):
                 nc.tensor.transpose(out=pa[:, t, :], in_=a_bf[b][:, t * P:(t + 1) * P], identity=ident_bf[:])
-            nc.scalar.copy(out=a_g[:, b * P:(b + 1) * P, :], in_=pa[:].rearrange("q t r -> q r t"))
-        regroup(nc.vector.tensor_copy, 0)
-        regroup(nc.scalar.copy, 1)
-        regroup(nc.scalar.copy, 2)
-        quant(f_g[0], f_q[0], f_s[0])
-        quant(a_g, a_q, a_s)
+            pas.append(pa)
+            if EXIT_ENGINE[b] == "S":
+                a_exit(b)
+        for g in range(NG):
+            if RG_ENGINE[g] == "S":
+                regroup(g)
+        quant0(0)
+        a_quant(0)
+        a_quant(1)
+        a_exit(3)
+        a_quant(2)
+        a_quant(3)
+        state["a_ready"] = 1
+        feed()
+        quant0(1)
+        quant0(2)
 
-        for j in range(4):
-            mx(1, j)
-        quant(f_g[1], f_q[1], f_s[1])
-        for j in range(4):
-            red(1, j)
-            mx(1, j + 4)
-        spread1(0)
-        quant(f_g[2], f_q[2], f_s[2])
-        for j in range(4, 8):
-            red(1, j)
-            mx(1, j + 4)
-        spread1(1)
-        facts1(0)
-        red(1, 8)
-        quant(g_g[0], g_q[0], g_s[0])
-        mx(2, 0)
-        for j in range(9, 12):
-            red(1, j)
-            mx(2, j - 8)
-        spread1(2)
-        facts1(1)
-        red(2, 0)
-        quant(g_g[1], g_q[1], g_s[1])
-        mx(2, 4)
-        for j in range(1, 4):
-            red(2, j)
-            mx(2, j + 4)
-        spread2(0)
-        facts1(2)
-        red(2, 4)
-        quant(g_g[2], g_q[2], g_s[2])
-        mx(2, 8)
-        for j in range(5, 8):
-            red(2, j)
-            mx(2, j + 4)
-        spread2(1)
-        final(0, 0, T)
-        for j in range(8, 12):
-            red(2, j)
-        spread2(2)
-        final(1, 0, T)
-        for t in range(T):
-            final(2, t, t + 1)
+        for i in range(NG + 2):
+            if i < NG and FINAL_MODE[i] != "D":
+                later(FLIP_AT, flip_facts, i)
+            if i < NG:
+                red(1, BPG * i)
+                red(1, BPG * i + 1)
+            if 0 <= i - 1 < NG:
+                facts1(i - 1)
+            if i < NG:
+                round1(i)
+                spread1(i)
+            if i == NG:
+                quant1(i - 1)
+            if 0 <= i - 2 < NG:
+                red(2, BPG * (i - 2))
+            if i - 3 >= 0 and FINAL_MODE[i - 3] == "D":
+                final_direct(i - 3, [0])
+            if 0 <= i - 1 < NG - 1:
+                quant1(i - 1)
+            if 0 <= i - 2 < NG:
+                red(2, BPG * (i - 2) + 1)
+                final_max(i - 2)
+                if FINAL_MODE[i - 2] != "D":
+                    for jj in range(BPG):
+                        later(RIPE[jj], final_flip, (i - 2, jj))
+            if i + 3 < NG:
+                quant0(i + 3)
+            if i - 3 >= 0 and FINAL_MODE[i - 3] == "D":
+                final_direct(i - 3, [2])
+        while waiting:
+            waiting.pop(0)[1]()
+        final_direct(NG - 1, [0, 2])

@@ -11,32 +11,21 @@ U8 = mybir.dt.uint8
 MAX = mybir.AluOpType.max
 MIN = mybir.AluOpType.min
 MULT = mybir.AluOpType.mult
-ADD = mybir.AluOpType.add
 AX = mybir.AxisListType.X
 EXP = mybir.ActivationFunctionType.Exp
 
 P = 128
 T = 4
 R = 512
+RB = R // P
 C = 1536
-CH = 512
-NCH = C // CH
 GW = 256
 NG = C // GW
 BPG = GW // P
-GPC = CH // GW
-BIG = 3.0e38
 
 FLOPS = 2 * 2 * 512 * 512 * 1536
 
-FINAL_MODE = ["G", "G", "G", "G", "D", "D"]
-RG_ENGINE = ["G", "G", "S", "S", "S", "S"]
-EXIT_ENGINE = ["S", "S", "S", "V"]
-ACC_BUFS = 4
-CV_ENGINE = "V"
-RIPE = [2, 3]
-FLIP_AT = 0
-ROWMAX_2X = True
+V_REGROUPS = 2
 
 
 def tile_differentiableilp_pa_kernel(tc, initial_facts, rule_weights, out):
@@ -46,27 +35,26 @@ def tile_differentiableilp_pa_kernel(tc, initial_facts, rule_weights, out):
 
     with ExitStack() as ctx:
         sb = ctx.enter_context(tc.tile_pool(name="sb", bufs=1))
-        rot = ctx.enter_context(tc.tile_pool(name="rot", bufs=4))
-        ps_acc = ctx.enter_context(tc.psum_pool(name="psacc", bufs=ACC_BUFS))
-        ps_b1 = ctx.enter_context(tc.psum_pool(name="psb1", bufs=1))
-        ps_tr = ctx.enter_context(tc.psum_pool(name="pstr", bufs=1))
-        ps_o = ctx.enter_context(tc.psum_pool(name="pso", bufs=2))
+        ps_s1 = ctx.enter_context(tc.psum_pool(name="ps_s1", bufs=2))
+        ps_s2 = ctx.enter_context(tc.psum_pool(name="ps_s2", bufs=2))
+        ps_b1 = ctx.enter_context(tc.psum_pool(name="ps_b1", bufs=1))
+        ps_tr = ctx.enter_context(tc.psum_pool(name="ps_tr", bufs=1))
+        ps_o = ctx.enter_context(tc.psum_pool(name="ps_o", bufs=2))
         ctx.enter_context(tc.manual_schedule())
 
-        w_sb = [sb.tile([P, R], BF16, name="w_sb%d" % b) for b in range(4)]
-        f_first = [sb.tile([P, T, GW], BF16, name="f_first%d" % h) for h in range(GPC)]
-        f_sb = [sb.tile([P, T, CH], BF16, name="f_sb%d" % k) for k in range(1, NCH)]
+        w_sb = [sb.tile([P, R], BF16, name="w_sb%d" % b) for b in range(RB)]
+        f_sb = [sb.tile([P, T, GW], BF16, name="f_sb%d" % g) for g in range(NG)]
         ident_bf = sb.tile([P, P], BF16, name="ident_bf")
         ident_f = sb.tile([P, P], F32, name="ident_f")
         dup = sb.tile([P, P, 2], BF16, name="dup")
         w_neg = sb.tile([P, R], BF16, name="w_neg")
         warm = sb.tile([P, 2], F32, name="warm")
-        nmax = sb.tile([P, 4], F32, name="nmax")
-        ssum = sb.tile([P, 4], F32, name="ssum")
-        rsum = sb.tile([P, 4], F32, name="rsum")
-        e_sb = [sb.tile([P, R], F32, name="e_sb%d" % b) for b in range(4)]
-        a_bf = [sb.tile([P, R], BF16, name="a_bf%d" % b) for b in range(4)]
-        a_g = [sb.tile([P, P, T], BF16, name="a_g%d" % b, align_bytes=64) for b in range(4)]
+        nmax = sb.tile([P, RB], F32, name="nmax")
+        ssum = sb.tile([P, RB], F32, name="ssum")
+        rsum = sb.tile([P, RB], F32, name="rsum")
+        e_sb = [sb.tile([P, R], F32, name="e_sb%d" % b) for b in range(RB)]
+        a_bf = [sb.tile([P, R], BF16, name="a_bf%d" % b) for b in range(RB)]
+        a_g = [sb.tile([P, P, T], BF16, name="a_g%d" % b, align_bytes=64) for b in range(RB)]
         a_q = sb.tile([P, R], U32, name="a_q", align_bytes=64)
         a_s = sb.tile([P, R], U8, name="a_s", align_bytes=64)
         f_g = [sb.tile([P, GW, T], BF16, name="f_g%d" % g, align_bytes=64) for g in range(NG)]
@@ -78,22 +66,15 @@ def tile_differentiableilp_pa_kernel(tc, initial_facts, rule_weights, out):
         m1 = [sb.tile([P, BPG], F32, name="m1_%d" % g) for g in range(NG)]
         m1b = [sb.tile([P, BPG], BF16, name="m1b_%d" % g) for g in range(NG)]
         m2 = [sb.tile([P, BPG], F32, name="m2_%d" % g) for g in range(NG)]
-        mm = [sb.tile([P, BPG], F32, name="mm_%d" % g) for g in range(NG)]
         f_t = [sb.tile([P, BPG, R], BF16, name="f_t%d" % g) for g in range(NG)]
-        o_sb = [sb.tile([P, T, GW], F32, name="o_sb%d" % g) for g in range(NG)]
+        o_t = [sb.tile([P, BPG, R], F32, name="o_t%d" % g) for g in range(NG)]
+        o_sb = [sb.tile([P, T, GW], F32, name="o_sb%d" % g) for g in range(NG - 1)]
+        o_end = [sb.tile([P, T, P], F32, name="o_end%d" % jj) for jj in range(BPG)]
 
-        def fsl(g):
-            k, h = divmod(g, GPC)
-            if k == 0:
-                return f_first[h][:]
-            return f_sb[k - 1][:, :, h * GW:(h + 1) * GW]
-
-        for b in range(4):
+        for b in range(RB):
             nc.sync.dma_start(out=w_sb[b][:], in_=rule_weights[b * P:(b + 1) * P, :])
-        for h in range(GPC):
-            nc.sync.dma_start(out=f_first[h][:], in_=facts_v[:, :, h * GW:(h + 1) * GW])
-        for k in range(1, NCH):
-            nc.sync.dma_start(out=f_sb[k - 1][:], in_=facts_v[:, :, k * CH:(k + 1) * CH])
+        for g in range(NG):
+            nc.sync.dma_start(out=f_sb[g][:], in_=facts_v[:, :, g * GW:(g + 1) * GW])
 
         nc.vector.memset(warm[:], 0.0)
         nc.scalar.activation(out=warm[:, 1:2], in_=warm[:, 0:1], func=EXP)
@@ -101,31 +82,19 @@ def tile_differentiableilp_pa_kernel(tc, initial_facts, rule_weights, out):
         make_identity(nc, ident_f[:])
         nc.gpsimd.tensor_copy(out=dup[:], in_=ident_bf[:].unsqueeze(2).to_broadcast([P, P, 2]))
 
-        def regroup(g):
-            dst = f_g[g][:].rearrange("p (c i) t -> p c t i", i=4)
-            src = fsl(g).rearrange("p t (c i) -> p c t i", i=4)
-            if RG_ENGINE[g] == "G":
-                nc.gpsimd.tensor_scalar(out=dst, in0=src, scalar1=1.0, scalar2=0.0, op0=MULT, op1=ADD)
-            elif RG_ENGINE[g] == "S":
-                nc.scalar.copy(out=dst, in_=src)
-            else:
-                nc.vector.tensor_copy(out=dst, in_=src)
+        def regroup(copy, g):
+            copy(
+                out=f_g[g][:].rearrange("p (c i) t -> p c t i", i=4),
+                in_=f_sb[g][:].rearrange("p t (c i) -> p c t i", i=4),
+            )
 
-        def quant(src, q, s):
+        def quantise(src, q, s):
             nc.vector.quantize_mx(out=q.bitcast(FP8X4), scales=s, in_=src.rearrange("p c t -> p (c t)"))
 
-        acc = {}
-        quantised = set()
-        order = []
-        state = {"next": 0, "open": 0, "a_ready": 0, "reds": 0}
-        waiting = []
-
-        def mx(step, j):
-            g, jj = divmod(j, BPG)
-            q, s = (f_q[g], f_s[g]) if step == 1 else (g_q[g], g_s[g])
-            a = ps_acc.tile([P, R], F32, name="acc%d_%d" % (step, j), tag="acc")
+        def one_pass(pool, q, s, jj):
+            acc = pool.tile([P, R], F32, name="acc", tag="acc")
             nc.tensor.matmul_mx(
-                out=a[:],
+                out=acc[:],
                 lhsT=q[:, jj * P:(jj + 1) * P].bitcast(FP8X4),
                 lhsT_scale=s[:, jj * P:(jj + 1) * P],
                 rhs=a_q[:].bitcast(FP8X4),
@@ -133,39 +102,10 @@ def tile_differentiableilp_pa_kernel(tc, initial_facts, rule_weights, out):
                 start=True,
                 stop=True,
             )
-            acc[(step, j)] = a
+            return acc
 
-        def feed():
-            while state["a_ready"] and state["next"] < len(order) and state["open"] < ACC_BUFS:
-                step, j = order[state["next"]]
-                if (step, j // BPG) not in quantised:
-                    break
-                mx(step, j)
-                state["next"] += 1
-                state["open"] += 1
-
-        def fill():
-            for n in range(len(waiting)):
-                if waiting[n][0] <= state["reds"]:
-                    waiting.pop(n)[1]()
-                    return
-
-        def red(step, j):
-            g, jj = divmod(j, BPG)
-            m = m1[g] if step == 1 else m2[g]
-            nc.vector.tensor_reduce(out=m[:, jj:jj + 1], in_=acc[(step, j)][:], axis=AX, op=MAX)
-            state["open"] -= 1
-            state["reds"] += 1
-            feed()
-            fill()
-
-        pb1 = {}
-
-        def round1(g):
-            if CV_ENGINE == "S":
-                nc.scalar.copy(out=m1b[g][:], in_=m1[g][:])
-            else:
-                nc.vector.tensor_copy(out=m1b[g][:], in_=m1[g][:])
+        def best_rule(acc, m, jj):
+            nc.vector.tensor_reduce(out=m[:, jj:jj + 1], in_=acc[:], axis=AX, op=MAX)
 
         def spread1(g):
             pb = ps_b1.tile([P, GW, 2], BF16, name="pb1_%d" % g, tag="pb1")
@@ -177,177 +117,103 @@ def tile_differentiableilp_pa_kernel(tc, initial_facts, rule_weights, out):
                     start=True,
                     stop=True,
                 )
-            pb1[g] = pb
+            return pb
 
-        def facts1(g):
+        def facts1(g, pb):
             nc.vector.tensor_tensor(
                 out=g_g[g][:].rearrange("p c (u e) -> p c u e", e=2),
                 in0=f_g[g][:].rearrange("p c (u e) -> p c u e", e=2),
-                in1=pb1[g][:].unsqueeze(2).to_broadcast([P, GW, 2, 2]),
+                in1=pb[:].unsqueeze(2).to_broadcast([P, GW, 2, 2]),
                 op=MAX,
             )
 
-        def quant1(g):
-            quant(g_g[g][:], g_q[g][:], g_s[g][:])
-            quantised.add((2, g))
-            feed()
-
-        def quant0(g):
-            quant(f_g[g][:], f_q[g][:], f_s[g][:])
-            quantised.add((1, g))
-            feed()
-
         def flip_facts(g):
             pf = ps_tr.tile([P, BPG, R], BF16, name="pf%d" % g, tag="tr")
-            src = fsl(g)
             for jj in range(BPG):
                 for t in range(T):
                     nc.tensor.transpose(
-                        out=pf[:, jj, t * P:(t + 1) * P], in_=src[:, t, jj * P:(jj + 1) * P], identity=ident_bf[:]
+                        out=pf[:, jj, t * P:(t + 1) * P], in_=f_sb[g][:, t, jj * P:(jj + 1) * P], identity=ident_bf[:]
                     )
             nc.scalar.copy(out=f_t[g][:], in_=pf[:])
 
-        ots = {}
-
-        def final_max(g):
-            mode = FINAL_MODE[g]
-            if mode == "D":
-                nc.vector.tensor_tensor(out=mm[g][:], in0=m1[g][:], in1=m2[g][:], op=MAX)
-                if g % 2 == 0:
-                    pb = ps_tr.tile([P, GW], F32, name="pb2_%d" % g, tag="tr")
-                else:
-                    pb = ps_b1.tile([P, GW], F32, name="pb2_%d" % g, tag="pb1")
-                for jj in range(BPG):
-                    nc.tensor.transpose(
-                        out=pb[:, jj * P:(jj + 1) * P],
-                        in_=mm[g][:, jj:jj + 1].to_broadcast([P, P]),
-                        identity=ident_f[:],
-                    )
-                ots[g] = pb
-                return
+        def last_flipped(g):
             for jj in range(BPG):
-                ot = rot.tile([P, R], F32, name="ot%d_%d" % (g, jj), tag="ot")
-                if mode == "G":
-                    nc.gpsimd.tensor_scalar(
-                        out=mm[g][:, jj:jj + 1], in0=m2[g][:, jj:jj + 1], scalar1=BIG,
-                        scalar2=m1[g][:, jj:jj + 1], op0=MIN, op1=MAX,
-                    )
-                    nc.gpsimd.tensor_scalar(
-                        out=ot[:], in0=f_t[g][:, jj, :], scalar1=BIG, scalar2=mm[g][:, jj:jj + 1], op0=MIN, op1=MAX
-                    )
-                else:
-                    nc.vector.tensor_scalar(
-                        out=ot[:], in0=f_t[g][:, jj, :], scalar1=m1[g][:, jj:jj + 1],
-                        scalar2=m2[g][:, jj:jj + 1], op0=MAX, op1=MAX,
-                    )
-                ots[(g, jj)] = ot
-
-        def final_direct(g, halves):
-            for t0 in halves:
-                nc.vector.tensor_tensor(
-                    out=o_sb[g][:, t0:t0 + 2, :],
-                    in0=fsl(g)[:, t0:t0 + 2, :],
-                    in1=ots[g][:].unsqueeze(1).to_broadcast([P, 2, GW]),
-                    op=MAX,
+                nc.vector.tensor_scalar(
+                    out=o_t[g][:, jj, :], in0=f_t[g][:, jj, :], scalar1=m1[g][:, jj:jj + 1],
+                    scalar2=m2[g][:, jj:jj + 1], op0=MAX, op1=MAX,
                 )
-                nc.sync.dma_start(out=out_v[:, t0:t0 + 2, g * GW:(g + 1) * GW], in_=o_sb[g][:, t0:t0 + 2, :])
-
-        def final_flip(gj):
-            g, jj = gj
-            po = ps_o.tile([P, T, P], F32, name="po%d_%d" % (g, jj), tag="po")
-            for t in range(T):
-                nc.tensor.transpose(out=po[:, t, :], in_=ots[(g, jj)][:, t * P:(t + 1) * P], identity=ident_f[:])
-            nc.scalar.copy(out=o_sb[g][:, :, jj * P:(jj + 1) * P], in_=po[:])
-            if jj == BPG - 1:
+            for jj in range(BPG):
+                po = ps_o.tile([P, T, P], F32, name="po%d_%d" % (g, jj), tag="po")
+                for t in range(T):
+                    nc.tensor.transpose(out=po[:, t, :], in_=o_t[g][:, jj, t * P:(t + 1) * P], identity=ident_f[:])
+                if g < NG - 1:
+                    nc.scalar.copy(out=o_sb[g][:, :, jj * P:(jj + 1) * P], in_=po[:])
+                else:
+                    leave = nc.scalar.copy if jj == 0 else nc.vector.tensor_copy
+                    leave(out=o_end[jj][:], in_=po[:])
+                    c0 = g * GW + jj * P
+                    nc.sync.dma_start(out=out_v[:, :, c0:c0 + P], in_=o_end[jj][:])
+            if g < NG - 1:
                 nc.sync.dma_start(out=out_v[:, :, g * GW:(g + 1) * GW], in_=o_sb[g][:])
 
-        def later(delay, fn, g):
-            waiting.append((state["reds"] + delay, lambda: fn(g)))
-
-        for i in range(NG + 2):
-            if i < NG:
-                order.extend([(1, BPG * i + jj) for jj in range(BPG)])
-            if 0 <= i - 2 < NG:
-                order.extend([(2, BPG * (i - 2) + jj) for jj in range(BPG)])
-
-        for b in range(4):
-            if ROWMAX_2X:
-                nc.vector.tensor_scalar(
-                    out=w_neg[:], in0=w_sb[b][:], scalar1=-1.0, scalar2=None, op0=MULT, op1=MIN,
-                    accum_out=nmax[:, b:b + 1],
-                )
-            else:
-                nc.vector.tensor_reduce(out=nmax[:, b:b + 1], in_=w_sb[b][:], axis=AX, op=MAX, negate=True)
+        for b in range(RB):
+            nc.vector.tensor_scalar(
+                out=w_neg[:], in0=w_sb[b][:], scalar1=-1.0, scalar2=None, op0=MULT, op1=MIN,
+                accum_out=nmax[:, b:b + 1],
+            )
             nc.scalar.activation(
                 out=e_sb[b][:], in_=w_sb[b][:], func=EXP, bias=nmax[:, b:b + 1], scale=1.0,
                 accum_out=ssum[:, b:b + 1],
             )
-        for g in range(NG):
-            if RG_ENGINE[g] == "G":
-                regroup(g)
         pas = []
-
-        def a_exit(bb):
-            cp = nc.scalar.copy if EXIT_ENGINE[bb] == "S" else nc.vector.tensor_copy
-            cp(out=a_g[bb][:], in_=pas[bb][:].rearrange("q t r -> q r t"))
-
-        def a_quant(bb):
-            quant(a_g[bb][:], a_q[:, bb * P:(bb + 1) * P], a_s[:, bb * P:(bb + 1) * P])
-
-        for b in range(4):
+        for b in range(RB):
             nc.vector.reciprocal(out=rsum[:, b:b + 1], in_=ssum[:, b:b + 1])
             nc.vector.tensor_scalar(
                 out=a_bf[b][:], in0=e_sb[b][:], scalar1=rsum[:, b:b + 1], scalar2=None, op0=MULT
             )
-            pa = ps_acc.tile([P, T, P], BF16, name="pa%d" % b, tag="acc")
+            pa = (ps_s1 if b < 2 else ps_s2).tile([P, T, P], BF16, name="pa%d" % b, tag="acc")
             for t in range(T):
                 nc.tensor.transpose(out=pa[:, t, :], in_=a_bf[b][:, t * P:(t + 1) * P], identity=ident_bf[:])
             pas.append(pa)
-            if EXIT_ENGINE[b] == "S":
-                a_exit(b)
-        for g in range(NG):
-            if RG_ENGINE[g] == "S":
-                regroup(g)
-        quant0(0)
-        a_quant(0)
-        a_quant(1)
-        a_exit(3)
-        a_quant(2)
-        a_quant(3)
-        state["a_ready"] = 1
-        feed()
-        quant0(1)
-        quant0(2)
+            if b < RB - 1:
+                nc.scalar.copy(out=a_g[b][:], in_=pa[:].rearrange("q t r -> q r t"))
+            if b == 0:
+                regroup(nc.vector.tensor_copy, 0)
+        for g in range(V_REGROUPS, NG):
+            regroup(nc.scalar.copy, g)
+        quantise(f_g[0][:], f_q[0][:], f_s[0][:])
+        for b in range(RB):
+            if b == RB - 2:
+                nc.vector.tensor_copy(out=a_g[RB - 1][:], in_=pas[RB - 1][:].rearrange("q t r -> q r t"))
+            quantise(a_g[b][:], a_q[:, b * P:(b + 1) * P], a_s[:, b * P:(b + 1) * P])
+        sums1 = [one_pass(ps_s1, f_q[0], f_s[0], jj) for jj in range(BPG)]
+        sums2 = [None, None]
+        spread = {}
+        for g in range(1, V_REGROUPS):
+            regroup(nc.vector.tensor_copy, g)
+        quantise(f_g[1][:], f_q[1][:], f_s[1][:])
 
         for i in range(NG + 2):
-            if i < NG and FINAL_MODE[i] != "D":
-                later(FLIP_AT, flip_facts, i)
+            for jj in range(BPG):
+                if i < NG:
+                    best_rule(sums1[jj], m1[i], jj)
+                if i + 1 < NG:
+                    sums1[jj] = one_pass(ps_s1, f_q[i + 1], f_s[i + 1], jj)
             if i < NG:
-                red(1, BPG * i)
-                red(1, BPG * i + 1)
+                flip_facts(i)
             if 0 <= i - 1 < NG:
-                facts1(i - 1)
+                facts1(i - 1, spread[i - 1])
             if i < NG:
-                round1(i)
-                spread1(i)
-            if i == NG:
-                quant1(i - 1)
+                nc.vector.tensor_copy(out=m1b[i][:], in_=m1[i][:])
+                spread[i] = spread1(i)
+            for jj in range(BPG):
+                if 0 <= i - 2 < NG:
+                    best_rule(sums2[jj], m2[i - 2], jj)
+                if 0 <= i - 1 < NG:
+                    if jj == 0:
+                        quantise(g_g[i - 1][:], g_q[i - 1][:], g_s[i - 1][:])
+                    sums2[jj] = one_pass(ps_s2, g_q[i - 1], g_s[i - 1], jj)
             if 0 <= i - 2 < NG:
-                red(2, BPG * (i - 2))
-            if i - 3 >= 0 and FINAL_MODE[i - 3] == "D":
-                final_direct(i - 3, [0])
-            if 0 <= i - 1 < NG - 1:
-                quant1(i - 1)
-            if 0 <= i - 2 < NG:
-                red(2, BPG * (i - 2) + 1)
-                final_max(i - 2)
-                if FINAL_MODE[i - 2] != "D":
-                    for jj in range(BPG):
-                        later(RIPE[jj], final_flip, (i - 2, jj))
-            if i + 3 < NG:
-                quant0(i + 3)
-            if i - 3 >= 0 and FINAL_MODE[i - 3] == "D":
-                final_direct(i - 3, [2])
-        while waiting:
-            waiting.pop(0)[1]()
-        final_direct(NG - 1, [0, 2])
+                last_flipped(i - 2)
+            if i + 2 < NG:
+                quantise(f_g[i + 2][:], f_q[i + 2][:], f_s[i + 2][:])

@@ -26,12 +26,14 @@ BPG = GW // P
 FLOPS = 2 * 2 * 512 * 512 * 1536
 
 V_REGROUPS = 2
+NG_POOL = NG - 2
+BF16_MAX = 3.3895313892515355e38
 
 
 def tile_differentiableilp_pa_kernel(tc, initial_facts, rule_weights, out):
     nc = tc.nc
-    facts_v = initial_facts.rearrange("(t q) c -> q t c", q=P)
-    out_v = out.rearrange("(t q) c -> q t c", q=P)
+    facts_v = initial_facts.rearrange("(q t) c -> q t c", t=T)
+    out_v = out.rearrange("(q t) c -> q t c", t=T)
 
     with ExitStack() as ctx:
         sb = ctx.enter_context(tc.tile_pool(name="sb", bufs=1))
@@ -47,7 +49,7 @@ def tile_differentiableilp_pa_kernel(tc, initial_facts, rule_weights, out):
         ident_bf = sb.tile([P, P], BF16, name="ident_bf")
         ident_f = sb.tile([P, P], F32, name="ident_f")
         dup = sb.tile([P, P, 2], BF16, name="dup")
-        w_neg = sb.tile([P, R], BF16, name="w_neg")
+        w_neg = [sb.tile([P, R], BF16, name="w_neg%d" % b) for b in range(RB)]
         warm = sb.tile([P, 2], F32, name="warm")
         nmax = sb.tile([P, RB], F32, name="nmax")
         ssum = sb.tile([P, RB], F32, name="ssum")
@@ -66,6 +68,7 @@ def tile_differentiableilp_pa_kernel(tc, initial_facts, rule_weights, out):
         m1 = [sb.tile([P, BPG], F32, name="m1_%d" % g) for g in range(NG)]
         m1b = [sb.tile([P, BPG], BF16, name="m1b_%d" % g) for g in range(NG)]
         m2 = [sb.tile([P, BPG], F32, name="m2_%d" % g) for g in range(NG)]
+        m12 = [sb.tile([P, BPG], F32, name="m12_%d" % g) for g in range(NG)]
         f_t = [sb.tile([P, BPG, R], BF16, name="f_t%d" % g) for g in range(NG)]
         o_t = [sb.tile([P, BPG, R], F32, name="o_t%d" % g) for g in range(NG)]
         o_sb = [sb.tile([P, T, GW], F32, name="o_sb%d" % g) for g in range(NG - 1)]
@@ -80,13 +83,15 @@ def tile_differentiableilp_pa_kernel(tc, initial_facts, rule_weights, out):
         nc.scalar.activation(out=warm[:, 1:2], in_=warm[:, 0:1], func=EXP)
         make_identity(nc, ident_bf[:])
         make_identity(nc, ident_f[:])
-        nc.gpsimd.tensor_copy(out=dup[:], in_=ident_bf[:].unsqueeze(2).to_broadcast([P, P, 2]))
 
         def regroup(copy, g):
             copy(
                 out=f_g[g][:].rearrange("p (c i) t -> p c t i", i=4),
                 in_=f_sb[g][:].rearrange("p t (c i) -> p c t i", i=4),
             )
+
+        def words_of(tile):
+            return tile[:].rearrange("p r t -> p (r t)").bitcast(F32).rearrange("p (r u) -> p r u", u=2)
 
         def quantise(src, q, s):
             nc.vector.quantize_mx(out=q.bitcast(FP8X4), scales=s, in_=src.rearrange("p c t -> p (c t)"))
@@ -136,58 +141,108 @@ def tile_differentiableilp_pa_kernel(tc, initial_facts, rule_weights, out):
                     )
             nc.scalar.copy(out=f_t[g][:], in_=pf[:])
 
-        def last_flipped(g):
-            for jj in range(BPG):
-                nc.vector.tensor_scalar(
-                    out=o_t[g][:, jj, :], in0=f_t[g][:, jj, :], scalar1=m1[g][:, jj:jj + 1],
-                    scalar2=m2[g][:, jj:jj + 1], op0=MAX, op1=MAX,
-                )
-            for jj in range(BPG):
-                po = ps_o.tile([P, T, P], F32, name="po%d_%d" % (g, jj), tag="po")
-                for t in range(T):
-                    nc.tensor.transpose(out=po[:, t, :], in_=o_t[g][:, jj, t * P:(t + 1) * P], identity=ident_f[:])
-                if g < NG - 1:
-                    nc.scalar.copy(out=o_sb[g][:, :, jj * P:(jj + 1) * P], in_=po[:])
-                else:
-                    leave = nc.scalar.copy if jj == 0 else nc.vector.tensor_copy
-                    leave(out=o_end[jj][:], in_=po[:])
-                    c0 = g * GW + jj * P
-                    nc.sync.dma_start(out=out_v[:, :, c0:c0 + P], in_=o_end[jj][:])
-            if g < NG - 1:
-                nc.sync.dma_start(out=out_v[:, :, g * GW:(g + 1) * GW], in_=o_sb[g][:])
+        def best_of_both(g, jj):
+            nc.gpsimd.tensor_scalar(
+                out=m12[g][:, jj:jj + 1], in0=m2[g][:, jj:jj + 1], scalar1=m1[g][:, jj:jj + 1],
+                scalar2=None, op0=MAX,
+            )
 
-        for b in range(RB):
+        def last_max_pool(g):
+            for jj in range(BPG):
+                best_of_both(g, jj)
+            for jj in range(BPG):
+                nc.gpsimd.tensor_scalar(
+                    out=o_t[g][:, jj, :], in0=f_t[g][:, jj, :], scalar1=BF16_MAX,
+                    scalar2=m12[g][:, jj:jj + 1], op0=MIN, op1=MAX,
+                )
+
+        def last_max(g, jj):
             nc.vector.tensor_scalar(
-                out=w_neg[:], in0=w_sb[b][:], scalar1=-1.0, scalar2=None, op0=MULT, op1=MIN,
+                out=o_t[g][:, jj, :], in0=f_t[g][:, jj, :], scalar1=m1[g][:, jj:jj + 1],
+                scalar2=m2[g][:, jj:jj + 1], op0=MAX, op1=MAX,
+            )
+
+        def flip_back(g, jj, dest):
+            po = (ps_o if g < NG_POOL else ps_s1).tile([P, T, P], F32, name="po%d_%d" % (g, jj), tag="po" if g < NG_POOL else "acc")
+            for t in range(T):
+                nc.tensor.transpose(out=po[:, t, :], in_=o_t[g][:, jj, t * P:(t + 1) * P], identity=ident_f[:])
+            nc.scalar.copy(out=dest, in_=po[:])
+
+        def finish(g):
+            for jj in range(BPG):
+                flip_back(g, jj, o_sb[g][:, :, jj * P:(jj + 1) * P])
+            nc.sync.dma_start(out=out_v[:, :, g * GW:(g + 1) * GW], in_=o_sb[g][:])
+
+        def spread_end(jj):
+            g = NG - 1
+            best_of_both(g, jj)
+            pm = (ps_o if jj == 0 else ps_b1).tile([P, P], F32, name="pm%d" % jj, tag="po" if jj == 0 else "pb1")
+            nc.tensor.transpose(out=pm[:], in_=m12[g][:, jj:jj + 1].to_broadcast([P, P]), identity=ident_f[:])
+            return pm
+
+        def last_max_end(jj, pm):
+            nc.vector.tensor_tensor(
+                out=o_end[jj][:], in0=f_sb[NG - 1][:, :, jj * P:(jj + 1) * P],
+                in1=pm[:].unsqueeze(1).to_broadcast([P, T, P]), op=MAX,
+            )
+            c0 = (NG - 1) * GW + jj * P
+            nc.sync.dma_start(out=out_v[:, :, c0:c0 + P], in_=o_end[jj][:])
+
+        pas = {}
+
+        def row_max_exp(b):
+            nc.vector.tensor_scalar(
+                out=w_neg[b][:], in0=w_sb[b][:], scalar1=-1.0, scalar2=None, op0=MULT, op1=MIN,
                 accum_out=nmax[:, b:b + 1],
             )
             nc.scalar.activation(
                 out=e_sb[b][:], in_=w_sb[b][:], func=EXP, bias=nmax[:, b:b + 1], scale=1.0,
                 accum_out=ssum[:, b:b + 1],
             )
-        pas = []
-        for b in range(RB):
+
+        def inverse_sum(b):
             nc.vector.reciprocal(out=rsum[:, b:b + 1], in_=ssum[:, b:b + 1])
+
+        def normalise(b):
             nc.vector.tensor_scalar(
                 out=a_bf[b][:], in0=e_sb[b][:], scalar1=rsum[:, b:b + 1], scalar2=None, op0=MULT
             )
-            pa = (ps_s1 if b < 2 else ps_s2).tile([P, T, P], BF16, name="pa%d" % b, tag="acc")
-            for t in range(T):
-                nc.tensor.transpose(out=pa[:, t, :], in_=a_bf[b][:, t * P:(t + 1) * P], identity=ident_bf[:])
-            pas.append(pa)
-            if b < RB - 1:
-                nc.scalar.copy(out=a_g[b][:], in_=pa[:].rearrange("q t r -> q r t"))
-            if b == 0:
-                regroup(nc.vector.tensor_copy, 0)
+            words = a_bf[b][:].bitcast(F32)
+            pas[b] = (ps_s1 if b < 2 else ps_s2).tile([P, 2, P], F32, name="pa%d" % b, tag="acc")
+            for u in range(2):
+                nc.tensor.transpose(out=pas[b][:, u, :], in_=words[:, u::2], identity=ident_f[:])
+
+        def lay_words(copy, b):
+            copy(out=words_of(a_g[b]), in_=pas[b][:].rearrange("q u r -> q r u"))
+
+        def quantise_rules(b):
+            quantise(a_g[b][:], a_q[:, b * P:(b + 1) * P], a_s[:, b * P:(b + 1) * P])
+
+        for b in range(RB):
+            row_max_exp(b)
+        nc.gpsimd.tensor_copy(out=dup[:], in_=ident_bf[:].unsqueeze(2).to_broadcast([P, P, 2]))
+        inverse_sum(0)
+        inverse_sum(1)
+        normalise(0)
+        normalise(1)
+        inverse_sum(2)
+        regroup(nc.vector.tensor_copy, 0)
+        normalise(2)
+        inverse_sum(3)
+        quantise(f_g[0][:], f_q[0][:], f_s[0][:])
+        for b in range(RB - 1):
+            lay_words(nc.scalar.copy, b)
+        quantise_rules(0)
+        normalise(3)
+        quantise_rules(1)
+        lay_words(nc.vector.tensor_copy, 3)
+        quantise_rules(2)
+        quantise_rules(3)
         for g in range(V_REGROUPS, NG):
             regroup(nc.scalar.copy, g)
-        quantise(f_g[0][:], f_q[0][:], f_s[0][:])
-        for b in range(RB):
-            if b == RB - 2:
-                nc.vector.tensor_copy(out=a_g[RB - 1][:], in_=pas[RB - 1][:].rearrange("q t r -> q r t"))
-            quantise(a_g[b][:], a_q[:, b * P:(b + 1) * P], a_s[:, b * P:(b + 1) * P])
         sums1 = [one_pass(ps_s1, f_q[0], f_s[0], jj) for jj in range(BPG)]
         sums2 = [None, None]
+        ends = []
         spread = {}
         for g in range(1, V_REGROUPS):
             regroup(nc.vector.tensor_copy, g)
@@ -199,21 +254,32 @@ def tile_differentiableilp_pa_kernel(tc, initial_facts, rule_weights, out):
                     best_rule(sums1[jj], m1[i], jj)
                 if i + 1 < NG:
                     sums1[jj] = one_pass(ps_s1, f_q[i + 1], f_s[i + 1], jj)
-            if i < NG:
+            if i < NG - 1:
                 flip_facts(i)
             if 0 <= i - 1 < NG:
                 facts1(i - 1, spread[i - 1])
             if i < NG:
-                nc.vector.tensor_copy(out=m1b[i][:], in_=m1[i][:])
+                nc.gpsimd.tensor_copy(out=m1b[i][:], in_=m1[i][:])
+            if i < NG:
                 spread[i] = spread1(i)
             for jj in range(BPG):
                 if 0 <= i - 2 < NG:
                     best_rule(sums2[jj], m2[i - 2], jj)
+                    if i - 2 == NG - 1:
+                        ends.append(spread_end(jj))
                 if 0 <= i - 1 < NG:
                     if jj == 0:
                         quantise(g_g[i - 1][:], g_q[i - 1][:], g_s[i - 1][:])
                     sums2[jj] = one_pass(ps_s2, g_q[i - 1], g_s[i - 1], jj)
-            if 0 <= i - 2 < NG:
-                last_flipped(i - 2)
             if i + 2 < NG:
                 quantise(f_g[i + 2][:], f_q[i + 2][:], f_s[i + 2][:])
+            if 0 <= i - 3 < NG_POOL:
+                finish(i - 3)
+            if 0 <= i - 2 < NG_POOL:
+                last_max_pool(i - 2)
+            elif NG_POOL <= i - 2 < NG - 1:
+                for jj in range(BPG):
+                    last_max(i - 2, jj)
+                finish(i - 2)
+        for jj in range(BPG):
+            last_max_end(jj, ends[jj])

@@ -25,7 +25,8 @@ BPG = GW // P
 
 FLOPS = 2 * 2 * 512 * 512 * 1536
 
-V_REGROUPS = 2
+V_REGROUPS = 1
+HEAD_REGROUPS = 4
 NG_POOL = NG - 2
 BF16_MAX = 3.3895313892515355e38
 
@@ -69,10 +70,10 @@ def tile_differentiableilp_pa_kernel(tc, initial_facts, rule_weights, out):
         m1b = [sb.tile([P, BPG], BF16, name="m1b_%d" % g) for g in range(NG)]
         m2 = [sb.tile([P, BPG], F32, name="m2_%d" % g) for g in range(NG)]
         m12 = [sb.tile([P, BPG], F32, name="m12_%d" % g) for g in range(NG)]
-        f_t = [sb.tile([P, BPG, R], BF16, name="f_t%d" % g) for g in range(NG)]
-        o_t = [sb.tile([P, BPG, R], F32, name="o_t%d" % g) for g in range(NG)]
-        o_sb = [sb.tile([P, T, GW], F32, name="o_sb%d" % g) for g in range(NG - 1)]
-        o_end = [sb.tile([P, T, P], F32, name="o_end%d" % jj) for jj in range(BPG)]
+        f_t = [sb.tile([P, BPG, R], BF16, name="f_t%d" % g) for g in range(NG_POOL)]
+        o_t = [sb.tile([P, BPG, R], F32, name="o_t%d" % g) for g in range(NG_POOL)]
+        o_sb = [sb.tile([P, T, GW], F32, name="o_sb%d" % g) for g in range(NG_POOL)]
+        o_end = [[sb.tile([P, T, P], F32, name="o_end%d_%d" % (g, jj)) for jj in range(BPG)] for g in range(NG_POOL, NG)]
 
         for b in range(RB):
             nc.sync.dma_start(out=w_sb[b][:], in_=rule_weights[b * P:(b + 1) * P, :])
@@ -141,29 +142,20 @@ def tile_differentiableilp_pa_kernel(tc, initial_facts, rule_weights, out):
                     )
             nc.scalar.copy(out=f_t[g][:], in_=pf[:])
 
-        def best_of_both(g, jj):
-            nc.gpsimd.tensor_scalar(
-                out=m12[g][:, jj:jj + 1], in0=m2[g][:, jj:jj + 1], scalar1=m1[g][:, jj:jj + 1],
-                scalar2=None, op0=MAX,
-            )
-
         def last_max_pool(g):
             for jj in range(BPG):
-                best_of_both(g, jj)
+                nc.gpsimd.tensor_scalar(
+                    out=m12[g][:, jj:jj + 1], in0=m2[g][:, jj:jj + 1], scalar1=m1[g][:, jj:jj + 1],
+                    scalar2=None, op0=MAX,
+                )
             for jj in range(BPG):
                 nc.gpsimd.tensor_scalar(
                     out=o_t[g][:, jj, :], in0=f_t[g][:, jj, :], scalar1=BF16_MAX,
                     scalar2=m12[g][:, jj:jj + 1], op0=MIN, op1=MAX,
                 )
 
-        def last_max(g, jj):
-            nc.vector.tensor_scalar(
-                out=o_t[g][:, jj, :], in0=f_t[g][:, jj, :], scalar1=m1[g][:, jj:jj + 1],
-                scalar2=m2[g][:, jj:jj + 1], op0=MAX, op1=MAX,
-            )
-
         def flip_back(g, jj, dest):
-            po = (ps_o if g < NG_POOL else ps_s1).tile([P, T, P], F32, name="po%d_%d" % (g, jj), tag="po" if g < NG_POOL else "acc")
+            po = ps_o.tile([P, T, P], F32, name="po%d_%d" % (g, jj), tag="po")
             for t in range(T):
                 nc.tensor.transpose(out=po[:, t, :], in_=o_t[g][:, jj, t * P:(t + 1) * P], identity=ident_f[:])
             nc.scalar.copy(out=dest, in_=po[:])
@@ -171,22 +163,26 @@ def tile_differentiableilp_pa_kernel(tc, initial_facts, rule_weights, out):
         def finish(g):
             for jj in range(BPG):
                 flip_back(g, jj, o_sb[g][:, :, jj * P:(jj + 1) * P])
+
+        def store(g):
             nc.sync.dma_start(out=out_v[:, :, g * GW:(g + 1) * GW], in_=o_sb[g][:])
 
-        def spread_end(jj):
-            g = NG - 1
-            best_of_both(g, jj)
-            pm = (ps_o if jj == 0 else ps_b1).tile([P, P], F32, name="pm%d" % jj, tag="po" if jj == 0 else "pb1")
-            nc.tensor.transpose(out=pm[:], in_=m12[g][:, jj:jj + 1].to_broadcast([P, P]), identity=ident_f[:])
-            return pm
-
-        def last_max_end(jj, pm):
+        def last_spread(g, jj):
             nc.vector.tensor_tensor(
-                out=o_end[jj][:], in0=f_sb[NG - 1][:, :, jj * P:(jj + 1) * P],
-                in1=pm[:].unsqueeze(1).to_broadcast([P, T, P]), op=MAX,
+                out=m12[g][:, jj:jj + 1], in0=m1[g][:, jj:jj + 1], in1=m2[g][:, jj:jj + 1], op=MAX
             )
-            c0 = (NG - 1) * GW + jj * P
-            nc.sync.dma_start(out=out_v[:, :, c0:c0 + P], in_=o_end[jj][:])
+            pool, tag = ((ps_b1, "pb1") if jj == 0 else (ps_tr, "tr")) if g < NG - 1 else (ps_s1, "acc")
+            pm = pool.tile([P, P], F32, name="pm%d_%d" % (g, jj), tag=tag)
+            nc.tensor.transpose(out=pm[:], in_=m12[g][:, jj:jj + 1].to_broadcast([P, P]), identity=ident_f[:])
+            ends[g, jj] = pm
+
+        def last_direct(g, jj):
+            nc.vector.tensor_tensor(
+                out=o_end[g - NG_POOL][jj][:], in0=f_sb[g][:, :, jj * P:(jj + 1) * P],
+                in1=ends[g, jj][:].unsqueeze(1).to_broadcast([P, T, P]), op=MAX,
+            )
+            c0 = g * GW + jj * P
+            nc.sync.dma_start(out=out_v[:, :, c0:c0 + P], in_=o_end[g - NG_POOL][jj][:])
 
         pas = {}
 
@@ -232,54 +228,66 @@ def tile_differentiableilp_pa_kernel(tc, initial_facts, rule_weights, out):
         quantise(f_g[0][:], f_q[0][:], f_s[0][:])
         for b in range(RB - 1):
             lay_words(nc.scalar.copy, b)
-        quantise_rules(0)
         normalise(3)
+        quantise_rules(0)
         quantise_rules(1)
         lay_words(nc.vector.tensor_copy, 3)
         quantise_rules(2)
         quantise_rules(3)
-        for g in range(V_REGROUPS, NG):
+        for g in range(V_REGROUPS, HEAD_REGROUPS):
             regroup(nc.scalar.copy, g)
         sums1 = [one_pass(ps_s1, f_q[0], f_s[0], jj) for jj in range(BPG)]
         sums2 = [None, None]
-        ends = []
+        ends = {}
         spread = {}
-        for g in range(1, V_REGROUPS):
-            regroup(nc.vector.tensor_copy, g)
         quantise(f_g[1][:], f_q[1][:], f_s[1][:])
 
-        for i in range(NG + 2):
+        for i in range(NG):
             for jj in range(BPG):
                 if i < NG:
                     best_rule(sums1[jj], m1[i], jj)
                 if i + 1 < NG:
                     sums1[jj] = one_pass(ps_s1, f_q[i + 1], f_s[i + 1], jj)
-            if i < NG - 1:
+            if i < NG_POOL:
                 flip_facts(i)
-            if 0 <= i - 1 < NG:
+            if i + HEAD_REGROUPS < NG:
+                regroup(nc.scalar.copy, i + HEAD_REGROUPS)
+            if i >= 3:
+                finish(i - 3)
+                store(i - 3)
+            if i >= 1:
                 facts1(i - 1, spread[i - 1])
             if i < NG:
                 nc.gpsimd.tensor_copy(out=m1b[i][:], in_=m1[i][:])
-            if i < NG:
                 spread[i] = spread1(i)
             for jj in range(BPG):
-                if 0 <= i - 2 < NG:
+                if i >= 2:
                     best_rule(sums2[jj], m2[i - 2], jj)
-                    if i - 2 == NG - 1:
-                        ends.append(spread_end(jj))
-                if 0 <= i - 1 < NG:
+                if i >= 1:
                     if jj == 0:
                         quantise(g_g[i - 1][:], g_q[i - 1][:], g_s[i - 1][:])
                     sums2[jj] = one_pass(ps_s2, g_q[i - 1], g_s[i - 1], jj)
             if i + 2 < NG:
                 quantise(f_g[i + 2][:], f_q[i + 2][:], f_s[i + 2][:])
-            if 0 <= i - 3 < NG_POOL:
-                finish(i - 3)
             if 0 <= i - 2 < NG_POOL:
                 last_max_pool(i - 2)
-            elif NG_POOL <= i - 2 < NG - 1:
-                for jj in range(BPG):
-                    last_max(i - 2, jj)
-                finish(i - 2)
-        for jj in range(BPG):
-            last_max_end(jj, ends[jj])
+
+        g = NG - 1
+        facts1(g, spread[g])
+        best_rule(sums2[0], m2[g - 1], 0)
+        quantise(g_g[g][:], g_q[g][:], g_s[g][:])
+        sums2[0] = one_pass(ps_s2, g_q[g], g_s[g], 0)
+        last_spread(g - 1, 0)
+        best_rule(sums2[1], m2[g - 1], 1)
+        sums2[1] = one_pass(ps_s2, g_q[g], g_s[g], 1)
+        finish(NG_POOL - 1)
+        last_direct(g - 1, 0)
+        best_rule(sums2[0], m2[g], 0)
+        last_spread(g - 1, 1)
+        best_rule(sums2[1], m2[g], 1)
+        last_spread(g, 0)
+        last_direct(g - 1, 1)
+        store(NG_POOL - 1)
+        last_spread(g, 1)
+        last_direct(g, 0)
+        last_direct(g, 1)

@@ -25,9 +25,8 @@ BPG = GW // P
 
 FLOPS = 2 * 2 * 512 * 512 * 1536
 
-V_REGROUPS = 1
 HEAD_REGROUPS = 4
-NG_POOL = NG - 2
+NG_POOL = NG - 3
 BF16_MAX = 3.3895313892515355e38
 
 
@@ -49,7 +48,6 @@ def tile_differentiableilp_pa_kernel(tc, initial_facts, rule_weights, out):
         f_sb = [sb.tile([P, T, GW], BF16, name="f_sb%d" % g) for g in range(NG)]
         ident_bf = sb.tile([P, P], BF16, name="ident_bf")
         ident_f = sb.tile([P, P], F32, name="ident_f")
-        dup = sb.tile([P, P, 2], BF16, name="dup")
         w_neg = [sb.tile([P, R], BF16, name="w_neg%d" % b) for b in range(RB)]
         warm = sb.tile([P, 2], F32, name="warm")
         nmax = sb.tile([P, RB], F32, name="nmax")
@@ -67,13 +65,13 @@ def tile_differentiableilp_pa_kernel(tc, initial_facts, rule_weights, out):
         g_q = [sb.tile([P, GW], U32, name="g_q%d" % g, align_bytes=64) for g in range(NG)]
         g_s = [sb.tile([P, GW], U8, name="g_s%d" % g, align_bytes=64) for g in range(NG)]
         m1 = [sb.tile([P, BPG], F32, name="m1_%d" % g) for g in range(NG)]
-        m1b = [sb.tile([P, BPG], BF16, name="m1b_%d" % g) for g in range(NG)]
+        m1p = [sb.tile([P, BPG, 2], BF16, name="m1p_%d" % g) for g in range(NG)]
         m2 = [sb.tile([P, BPG], F32, name="m2_%d" % g) for g in range(NG)]
         m12 = [sb.tile([P, BPG], F32, name="m12_%d" % g) for g in range(NG)]
-        f_t = [sb.tile([P, BPG, R], BF16, name="f_t%d" % g) for g in range(NG_POOL)]
-        o_t = [sb.tile([P, BPG, R], F32, name="o_t%d" % g) for g in range(NG_POOL)]
-        o_sb = [sb.tile([P, T, GW], F32, name="o_sb%d" % g) for g in range(NG_POOL)]
-        o_end = [[sb.tile([P, T, P], F32, name="o_end%d_%d" % (g, jj)) for jj in range(BPG)] for g in range(NG_POOL, NG)]
+        f_t = [sb.tile([P, BPG, R], BF16, name="f_t%d" % g) for g in range(NG - 1)]
+        o_t = [sb.tile([P, BPG, R], F32, name="o_t%d" % g) for g in range(NG - 1)]
+        o_sb = [sb.tile([P, T, GW], F32, name="o_sb%d" % g) for g in range(NG - 2)]
+        o_end = [[sb.tile([P, T, P], F32, name="o_end%d_%d" % (g, jj)) for jj in range(BPG)] for g in range(NG - 2, NG)]
 
         for b in range(RB):
             nc.sync.dma_start(out=w_sb[b][:], in_=rule_weights[b * P:(b + 1) * P, :])
@@ -115,13 +113,11 @@ def tile_differentiableilp_pa_kernel(tc, initial_facts, rule_weights, out):
 
         def spread1(g):
             pb = ps_b1.tile([P, GW, 2], BF16, name="pb1_%d" % g, tag="pb1")
+            words = pb[:].rearrange("p c e -> p (c e)").bitcast(F32)
+            pairs = m1p[g][:].rearrange("p j e -> p (j e)").bitcast(F32)
             for jj in range(BPG):
-                nc.tensor.matmul(
-                    out=pb[:, jj * P:(jj + 1) * P, :].rearrange("p c e -> p (c e)"),
-                    lhsT=m1b[g][:, jj:jj + 1].to_broadcast([P, P]),
-                    rhs=dup[:].rearrange("p c e -> p (c e)"),
-                    start=True,
-                    stop=True,
+                nc.tensor.transpose(
+                    out=words[:, jj * P:(jj + 1) * P], in_=pairs[:, jj:jj + 1].to_broadcast([P, P]), identity=ident_f[:]
                 )
             return pb
 
@@ -154,35 +150,47 @@ def tile_differentiableilp_pa_kernel(tc, initial_facts, rule_weights, out):
                     scalar2=m12[g][:, jj:jj + 1], op0=MIN, op1=MAX,
                 )
 
-        def flip_back(g, jj, dest):
-            po = ps_o.tile([P, T, P], F32, name="po%d_%d" % (g, jj), tag="po")
+        def last_max_vector(g, jj):
+            nc.vector.tensor_scalar(
+                out=o_t[g][:, jj, :], in0=f_t[g][:, jj, :], scalar1=m1[g][:, jj:jj + 1],
+                scalar2=m2[g][:, jj:jj + 1], op0=MAX, op1=MAX,
+            )
+
+        def flip_back(g, jj, pool, tag, dest):
+            po = pool.tile([P, T, P], F32, name="po%d_%d" % (g, jj), tag=tag)
             for t in range(T):
                 nc.tensor.transpose(out=po[:, t, :], in_=o_t[g][:, jj, t * P:(t + 1) * P], identity=ident_f[:])
             nc.scalar.copy(out=dest, in_=po[:])
 
         def finish(g):
             for jj in range(BPG):
-                flip_back(g, jj, o_sb[g][:, :, jj * P:(jj + 1) * P])
+                flip_back(g, jj, ps_o, "po", o_sb[g][:, :, jj * P:(jj + 1) * P])
+            store(g)
 
         def store(g):
             nc.sync.dma_start(out=out_v[:, :, g * GW:(g + 1) * GW], in_=o_sb[g][:])
 
-        def last_spread(g, jj):
+        def store_block(g, jj):
+            c0 = g * GW + jj * P
+            nc.sync.dma_start(out=out_v[:, :, c0:c0 + P], in_=o_end[g - (NG - 2)][jj][:])
+
+        def last_spread(jj):
+            g = NG - 1
             nc.vector.tensor_tensor(
                 out=m12[g][:, jj:jj + 1], in0=m1[g][:, jj:jj + 1], in1=m2[g][:, jj:jj + 1], op=MAX
             )
-            pool, tag = ((ps_b1, "pb1") if jj == 0 else (ps_tr, "tr")) if g < NG - 1 else (ps_s1, "acc")
-            pm = pool.tile([P, P], F32, name="pm%d_%d" % (g, jj), tag=tag)
+            pool, tag = (ps_b1, "pb1") if jj == 0 else (ps_tr, "tr")
+            pm = pool.tile([P, P], F32, name="pm%d" % jj, tag=tag)
             nc.tensor.transpose(out=pm[:], in_=m12[g][:, jj:jj + 1].to_broadcast([P, P]), identity=ident_f[:])
-            ends[g, jj] = pm
+            return pm
 
-        def last_direct(g, jj):
+        def last_direct(jj, pm):
+            g = NG - 1
             nc.vector.tensor_tensor(
-                out=o_end[g - NG_POOL][jj][:], in0=f_sb[g][:, :, jj * P:(jj + 1) * P],
-                in1=ends[g, jj][:].unsqueeze(1).to_broadcast([P, T, P]), op=MAX,
+                out=o_end[1][jj][:], in0=f_sb[g][:, :, jj * P:(jj + 1) * P],
+                in1=pm[:].unsqueeze(1).to_broadcast([P, T, P]), op=MAX,
             )
-            c0 = g * GW + jj * P
-            nc.sync.dma_start(out=out_v[:, :, c0:c0 + P], in_=o_end[g - NG_POOL][jj][:])
+            store_block(g, jj)
 
         pas = {}
 
@@ -208,39 +216,51 @@ def tile_differentiableilp_pa_kernel(tc, initial_facts, rule_weights, out):
             for u in range(2):
                 nc.tensor.transpose(out=pas[b][:, u, :], in_=words[:, u::2], identity=ident_f[:])
 
+        def warm_up(b):
+            idle = ps_o.tile([P, R], F32, name="idle", tag="po")
+            nc.tensor.matmul(out=idle[:], lhsT=ident_bf[:], rhs=w_sb[b][:], start=True, stop=True)
+
         def lay_words(copy, b):
             copy(out=words_of(a_g[b]), in_=pas[b][:].rearrange("q u r -> q r u"))
 
         def quantise_rules(b):
             quantise(a_g[b][:], a_q[:, b * P:(b + 1) * P], a_s[:, b * P:(b + 1) * P])
 
-        for b in range(RB):
-            row_max_exp(b)
-        nc.gpsimd.tensor_copy(out=dup[:], in_=ident_bf[:].unsqueeze(2).to_broadcast([P, P, 2]))
+        row_max_exp(0)
+        row_max_exp(1)
+        row_max_exp(2)
+        row_max_exp(3)
+        warm_up(0)
+        warm_up(1)
+        warm_up(2)
         inverse_sum(0)
         inverse_sum(1)
         normalise(0)
         normalise(1)
+        warm_up(3)
         inverse_sum(2)
         regroup(nc.vector.tensor_copy, 0)
         normalise(2)
+        warm_up(0)
         inverse_sum(3)
-        quantise(f_g[0][:], f_q[0][:], f_s[0][:])
-        for b in range(RB - 1):
-            lay_words(nc.scalar.copy, b)
         normalise(3)
+        lay_words(nc.scalar.copy, 0)
+        lay_words(nc.scalar.copy, 1)
+        lay_words(nc.scalar.copy, 2)
+        quantise(f_g[0][:], f_q[0][:], f_s[0][:])
+        warm_up(1)
         quantise_rules(0)
         quantise_rules(1)
         lay_words(nc.vector.tensor_copy, 3)
         quantise_rules(2)
         quantise_rules(3)
-        for g in range(V_REGROUPS, HEAD_REGROUPS):
-            regroup(nc.scalar.copy, g)
+        regroup(nc.scalar.copy, 1)
+        regroup(nc.scalar.copy, 2)
+        regroup(nc.scalar.copy, 3)
         sums1 = [one_pass(ps_s1, f_q[0], f_s[0], jj) for jj in range(BPG)]
-        sums2 = [None, None]
-        ends = {}
-        spread = {}
         quantise(f_g[1][:], f_q[1][:], f_s[1][:])
+        sums2 = [None, None]
+        spread = {}
 
         for i in range(NG):
             for jj in range(BPG):
@@ -248,17 +268,16 @@ def tile_differentiableilp_pa_kernel(tc, initial_facts, rule_weights, out):
                     best_rule(sums1[jj], m1[i], jj)
                 if i + 1 < NG:
                     sums1[jj] = one_pass(ps_s1, f_q[i + 1], f_s[i + 1], jj)
-            if i < NG_POOL:
+            if i < NG - 1:
                 flip_facts(i)
             if i + HEAD_REGROUPS < NG:
                 regroup(nc.scalar.copy, i + HEAD_REGROUPS)
-            if i >= 3:
+            if 0 <= i - 3 < NG_POOL:
                 finish(i - 3)
-                store(i - 3)
             if i >= 1:
                 facts1(i - 1, spread[i - 1])
             if i < NG:
-                nc.gpsimd.tensor_copy(out=m1b[i][:], in_=m1[i][:])
+                nc.gpsimd.tensor_copy(out=m1p[i][:], in_=m1[i][:].unsqueeze(2).to_broadcast([P, BPG, 2]))
                 spread[i] = spread1(i)
             for jj in range(BPG):
                 if i >= 2:
@@ -271,23 +290,27 @@ def tile_differentiableilp_pa_kernel(tc, initial_facts, rule_weights, out):
                 quantise(f_g[i + 2][:], f_q[i + 2][:], f_s[i + 2][:])
             if 0 <= i - 2 < NG_POOL:
                 last_max_pool(i - 2)
+            elif i - 2 >= NG_POOL:
+                for jj in range(BPG):
+                    last_max_vector(i - 2, jj)
+                finish(i - 2)
 
         g = NG - 1
         facts1(g, spread[g])
         best_rule(sums2[0], m2[g - 1], 0)
         quantise(g_g[g][:], g_q[g][:], g_s[g][:])
         sums2[0] = one_pass(ps_s2, g_q[g], g_s[g], 0)
-        last_spread(g - 1, 0)
         best_rule(sums2[1], m2[g - 1], 1)
         sums2[1] = one_pass(ps_s2, g_q[g], g_s[g], 1)
-        finish(NG_POOL - 1)
-        last_direct(g - 1, 0)
+        last_max_vector(g - 1, 0)
+        flip_back(g - 1, 0, ps_s1, "acc", o_end[0][0][:])
+        store_block(g - 1, 0)
+        last_max_vector(g - 1, 1)
+        flip_back(g - 1, 1, ps_s1, "acc", o_end[0][1][:])
+        store_block(g - 1, 1)
         best_rule(sums2[0], m2[g], 0)
-        last_spread(g - 1, 1)
         best_rule(sums2[1], m2[g], 1)
-        last_spread(g, 0)
-        last_direct(g - 1, 1)
-        store(NG_POOL - 1)
-        last_spread(g, 1)
-        last_direct(g, 0)
-        last_direct(g, 1)
+        pm0 = last_spread(0)
+        pm1 = last_spread(1)
+        last_direct(0, pm0)
+        last_direct(1, pm1)

@@ -70,8 +70,7 @@ def tile_differentiableilp_pa_kernel(tc, initial_facts, rule_weights, out):
         m12 = [sb.tile([P, BPG], F32, name="m12_%d" % g) for g in range(NG)]
         f_t = [sb.tile([P, BPG, R], BF16, name="f_t%d" % g) for g in range(NG - 1)]
         o_t = [sb.tile([P, BPG, R], F32, name="o_t%d" % g) for g in range(NG - 1)]
-        o_sb = [sb.tile([P, T, GW], F32, name="o_sb%d" % g) for g in range(NG - 2)]
-        o_end = [[sb.tile([P, T, P], F32, name="o_end%d_%d" % (g, jj)) for jj in range(BPG)] for g in range(NG - 2, NG)]
+        o_sb = [sb.tile([P, T, GW], F32, name="o_sb%d" % g) for g in range(NG)]
 
         for b in range(RB):
             nc.sync.dma_start(out=w_sb[b][:], in_=rule_weights[b * P:(b + 1) * P, :])
@@ -156,23 +155,23 @@ def tile_differentiableilp_pa_kernel(tc, initial_facts, rule_weights, out):
                 scalar2=m2[g][:, jj:jj + 1], op0=MAX, op1=MAX,
             )
 
-        def flip_back(g, jj, pool, tag, dest):
-            po = pool.tile([P, T, P], F32, name="po%d_%d" % (g, jj), tag=tag)
-            for t in range(T):
-                nc.tensor.transpose(out=po[:, t, :], in_=o_t[g][:, jj, t * P:(t + 1) * P], identity=ident_f[:])
-            nc.scalar.copy(out=dest, in_=po[:])
-
         def finish(g):
-            for jj in range(BPG):
-                flip_back(g, jj, ps_o, "po", o_sb[g][:, :, jj * P:(jj + 1) * P])
-            store(g)
+            for h in range(2):
+                po = ps_o.tile([P, 2, GW], F32, name="po%d_%d" % (g, h), tag="po")
+                for t in range(2):
+                    for jj in range(BPG):
+                        nc.tensor.transpose(
+                            out=po[:, t, jj * P:(jj + 1) * P],
+                            in_=o_t[g][:, jj, (2 * h + t) * P:(2 * h + t + 1) * P],
+                            identity=ident_f[:],
+                        )
+                nc.scalar.copy(out=o_sb[g][:, 2 * h:2 * h + 2, :], in_=po[:])
+                store_half(g, h)
 
-        def store(g):
-            nc.sync.dma_start(out=out_v[:, :, g * GW:(g + 1) * GW], in_=o_sb[g][:])
-
-        def store_block(g, jj):
-            c0 = g * GW + jj * P
-            nc.sync.dma_start(out=out_v[:, :, c0:c0 + P], in_=o_end[g - (NG - 2)][jj][:])
+        def store_half(g, h):
+            nc.sync.dma_start(
+                out=out_v[:, 2 * h:2 * h + 2, g * GW:(g + 1) * GW], in_=o_sb[g][:, 2 * h:2 * h + 2, :]
+            )
 
         def last_spread(jj):
             g = NG - 1
@@ -184,13 +183,13 @@ def tile_differentiableilp_pa_kernel(tc, initial_facts, rule_weights, out):
             nc.tensor.transpose(out=pm[:], in_=m12[g][:, jj:jj + 1].to_broadcast([P, P]), identity=ident_f[:])
             return pm
 
-        def last_direct(jj, pm):
+        def last_direct(h, jj, pm):
             g = NG - 1
             nc.vector.tensor_tensor(
-                out=o_end[1][jj][:], in0=f_sb[g][:, :, jj * P:(jj + 1) * P],
-                in1=pm[:].unsqueeze(1).to_broadcast([P, T, P]), op=MAX,
+                out=o_sb[g][:, 2 * h:2 * h + 2, jj * P:(jj + 1) * P],
+                in0=f_sb[g][:, 2 * h:2 * h + 2, jj * P:(jj + 1) * P],
+                in1=pm[:].unsqueeze(1).to_broadcast([P, 2, P]), op=MAX,
             )
-            store_block(g, jj)
 
         pas = {}
 
@@ -303,14 +302,13 @@ def tile_differentiableilp_pa_kernel(tc, initial_facts, rule_weights, out):
         best_rule(sums2[1], m2[g - 1], 1)
         sums2[1] = one_pass(ps_s2, g_q[g], g_s[g], 1)
         last_max_vector(g - 1, 0)
-        flip_back(g - 1, 0, ps_s1, "acc", o_end[0][0][:])
-        store_block(g - 1, 0)
         last_max_vector(g - 1, 1)
-        flip_back(g - 1, 1, ps_s1, "acc", o_end[0][1][:])
-        store_block(g - 1, 1)
+        finish(g - 1)
         best_rule(sums2[0], m2[g], 0)
-        best_rule(sums2[1], m2[g], 1)
         pm0 = last_spread(0)
+        best_rule(sums2[1], m2[g], 1)
         pm1 = last_spread(1)
-        last_direct(0, pm0)
-        last_direct(1, pm1)
+        for h in range(2):
+            last_direct(h, 0, pm0)
+            last_direct(h, 1, pm1)
+            store_half(g, h)

@@ -88,14 +88,30 @@ def tile_differentiableilp_pa_kernel(tc, initial_facts, rule_weights, out):
                 in_=f_sb[g][:].rearrange("p t (c i) -> p c t i", i=4),
             )
 
+        def pairs_of(tile):
+            return tile[:].rearrange("p j k -> p (j k)").bitcast(F32)
+
         def words_of(tile):
             return tile[:].rearrange("p r t -> p (r t)").bitcast(F32).rearrange("p (r u) -> p r u", u=2)
+
+        def regroup_block(g, jj):
+            cols = slice(jj * P, (jj + 1) * P)
+            nc.vector.tensor_copy(
+                out=f_g[g][:, cols, :].rearrange("p (c i) t -> p c t i", i=4),
+                in_=f_sb[g][:, :, cols].rearrange("p t (c i) -> p c t i", i=4),
+            )
+
+        def quantise_block(g, jj):
+            cols = slice(jj * P, (jj + 1) * P)
+            quantise(f_g[g][:, cols, :], f_q[g][:, cols], f_s[g][:, cols])
 
         def quantise(src, q, s):
             nc.vector.quantize_mx(out=q.bitcast(FP8X4), scales=s, in_=src.rearrange("p c t -> p (c t)"))
 
-        def one_pass(pool, q, s, jj):
+        def one_pass(pool, q, s, jj, warm=False):
             acc = pool.tile([P, R], F32, name="acc", tag="acc")
+            if warm:
+                nc.tensor.matmul(out=acc[:], lhsT=ident_bf[:], rhs=w_sb[0][:], start=True, stop=True)
             nc.tensor.matmul_mx(
                 out=acc[:],
                 lhsT=q[:, jj * P:(jj + 1) * P].bitcast(FP8X4),
@@ -135,7 +151,7 @@ def tile_differentiableilp_pa_kernel(tc, initial_facts, rule_weights, out):
                     nc.tensor.transpose(
                         out=pf[:, jj, t * P:(t + 1) * P], in_=f_sb[g][:, t, jj * P:(jj + 1) * P], identity=ident_bf[:]
                     )
-            nc.scalar.copy(out=f_t[g][:], in_=pf[:])
+            nc.scalar.copy(out=pairs_of(f_t[g]), in_=pairs_of(pf))
 
         def last_max_pool(g):
             for jj in range(BPG):
@@ -225,6 +241,7 @@ def tile_differentiableilp_pa_kernel(tc, initial_facts, rule_weights, out):
         def quantise_rules(b):
             quantise(a_g[b][:], a_q[:, b * P:(b + 1) * P], a_s[:, b * P:(b + 1) * P])
 
+        sums1 = [None, None]
         row_max_exp(0)
         row_max_exp(1)
         row_max_exp(2)
@@ -233,22 +250,20 @@ def tile_differentiableilp_pa_kernel(tc, initial_facts, rule_weights, out):
         warm_up(1)
         warm_up(2)
         inverse_sum(0)
-        inverse_sum(1)
         normalise(0)
+        inverse_sum(1)
         normalise(1)
-        warm_up(3)
         inverse_sum(2)
-        regroup(nc.vector.tensor_copy, 0)
+        regroup_block(0, 0)
         normalise(2)
-        warm_up(0)
         inverse_sum(3)
         normalise(3)
         lay_words(nc.scalar.copy, 0)
         lay_words(nc.scalar.copy, 1)
         lay_words(nc.scalar.copy, 2)
-        quantise(f_g[0][:], f_q[0][:], f_s[0][:])
-        warm_up(1)
+        quantise_block(0, 0)
         quantise_rules(0)
+        regroup_block(0, 1)
         quantise_rules(1)
         lay_words(nc.vector.tensor_copy, 3)
         quantise_rules(2)
@@ -256,7 +271,9 @@ def tile_differentiableilp_pa_kernel(tc, initial_facts, rule_weights, out):
         regroup(nc.scalar.copy, 1)
         regroup(nc.scalar.copy, 2)
         regroup(nc.scalar.copy, 3)
-        sums1 = [one_pass(ps_s1, f_q[0], f_s[0], jj) for jj in range(BPG)]
+        sums1[0] = one_pass(ps_s1, f_q[0], f_s[0], 0)
+        quantise_block(0, 1)
+        sums1[1] = one_pass(ps_s1, f_q[0], f_s[0], 1)
         quantise(f_g[1][:], f_q[1][:], f_s[1][:])
         sums2 = [None, None]
         spread = {}
@@ -284,7 +301,7 @@ def tile_differentiableilp_pa_kernel(tc, initial_facts, rule_weights, out):
                 if i >= 1:
                     if jj == 0:
                         quantise(g_g[i - 1][:], g_q[i - 1][:], g_s[i - 1][:])
-                    sums2[jj] = one_pass(ps_s2, g_q[i - 1], g_s[i - 1], jj)
+                    sums2[jj] = one_pass(ps_s2, g_q[i - 1], g_s[i - 1], jj, warm=jj == 1)
             if i + 2 < NG:
                 quantise(f_g[i + 2][:], f_q[i + 2][:], f_s[i + 2][:])
             if 0 <= i - 2 < NG_POOL:
@@ -300,7 +317,7 @@ def tile_differentiableilp_pa_kernel(tc, initial_facts, rule_weights, out):
         quantise(g_g[g][:], g_q[g][:], g_s[g][:])
         sums2[0] = one_pass(ps_s2, g_q[g], g_s[g], 0)
         best_rule(sums2[1], m2[g - 1], 1)
-        sums2[1] = one_pass(ps_s2, g_q[g], g_s[g], 1)
+        sums2[1] = one_pass(ps_s2, g_q[g], g_s[g], 1, warm=True)
         last_max_vector(g - 1, 0)
         last_max_vector(g - 1, 1)
         finish(g - 1)

@@ -73,7 +73,7 @@ def tile_differentiableilp_pa_kernel(tc, initial_facts, rule_weights, out):
         o_sb = [sb.tile([P, T, GW], F32, name="o_sb%d" % g) for g in range(NG)]
 
         for b in range(RB):
-            nc.sync.dma_start(out=w_sb[b][:], in_=rule_weights[b * P:(b + 1) * P, :])
+            (nc.sync if b % 2 == 0 else nc.scalar).dma_start(out=w_sb[b][:], in_=rule_weights[b * P:(b + 1) * P, :])
         for g in range(NG):
             nc.sync.dma_start(out=f_sb[g][:], in_=facts_v[:, :, g * GW:(g + 1) * GW])
 
@@ -108,10 +108,8 @@ def tile_differentiableilp_pa_kernel(tc, initial_facts, rule_weights, out):
         def quantise(src, q, s):
             nc.vector.quantize_mx(out=q.bitcast(FP8X4), scales=s, in_=src.rearrange("p c t -> p (c t)"))
 
-        def one_pass(pool, q, s, jj, warm=False):
+        def one_pass(pool, q, s, jj):
             acc = pool.tile([P, R], F32, name="acc", tag="acc")
-            if warm:
-                nc.tensor.matmul(out=acc[:], lhsT=ident_bf[:], rhs=w_sb[0][:], start=True, stop=True)
             nc.tensor.matmul_mx(
                 out=acc[:],
                 lhsT=q[:, jj * P:(jj + 1) * P].bitcast(FP8X4),
@@ -253,15 +251,18 @@ def tile_differentiableilp_pa_kernel(tc, initial_facts, rule_weights, out):
         normalise(0)
         inverse_sum(1)
         normalise(1)
+        warm_up(3)
         inverse_sum(2)
         regroup_block(0, 0)
         normalise(2)
+        warm_up(0)
         inverse_sum(3)
         normalise(3)
         lay_words(nc.scalar.copy, 0)
         lay_words(nc.scalar.copy, 1)
         lay_words(nc.scalar.copy, 2)
         quantise_block(0, 0)
+        warm_up(1)
         quantise_rules(0)
         regroup_block(0, 1)
         quantise_rules(1)
@@ -301,7 +302,7 @@ def tile_differentiableilp_pa_kernel(tc, initial_facts, rule_weights, out):
                 if i >= 1:
                     if jj == 0:
                         quantise(g_g[i - 1][:], g_q[i - 1][:], g_s[i - 1][:])
-                    sums2[jj] = one_pass(ps_s2, g_q[i - 1], g_s[i - 1], jj, warm=jj == 1)
+                    sums2[jj] = one_pass(ps_s2, g_q[i - 1], g_s[i - 1], jj)
             if i + 2 < NG:
                 quantise(f_g[i + 2][:], f_q[i + 2][:], f_s[i + 2][:])
             if 0 <= i - 2 < NG_POOL:
@@ -317,7 +318,7 @@ def tile_differentiableilp_pa_kernel(tc, initial_facts, rule_weights, out):
         quantise(g_g[g][:], g_q[g][:], g_s[g][:])
         sums2[0] = one_pass(ps_s2, g_q[g], g_s[g], 0)
         best_rule(sums2[1], m2[g - 1], 1)
-        sums2[1] = one_pass(ps_s2, g_q[g], g_s[g], 1, warm=True)
+        sums2[1] = one_pass(ps_s2, g_q[g], g_s[g], 1)
         last_max_vector(g - 1, 0)
         last_max_vector(g - 1, 1)
         finish(g - 1)

@@ -49,6 +49,7 @@ def tile_differentiableilp_pa_kernel(tc, initial_facts, rule_weights, out):
         ident_bf = sb.tile([P, P], BF16, name="ident_bf")
         ident_f = sb.tile([P, P], F32, name="ident_f")
         w_neg = [sb.tile([P, R], BF16, name="w_neg%d" % b) for b in range(RB)]
+        junk = sb.tile([P, R], BF16, name="junk")
         warm = sb.tile([P, 2], F32, name="warm")
         nmax = sb.tile([P, RB], F32, name="nmax")
         ssum = sb.tile([P, RB], F32, name="ssum")
@@ -124,6 +125,12 @@ def tile_differentiableilp_pa_kernel(tc, initial_facts, rule_weights, out):
         def best_rule(acc, m, jj):
             nc.vector.tensor_reduce(out=m[:, jj:jj + 1], in_=acc[:], axis=AX, op=MAX)
 
+        def best_of_steps(acc, g, jj):
+            nc.vector.tensor_scalar(
+                out=junk[:], in0=acc[:], scalar1=1.0, scalar2=m1[g][:, jj:jj + 1], op0=MULT, op1=MAX,
+                accum_out=m12[g][:, jj:jj + 1],
+            )
+
         def spread1(g):
             pb = ps_b1.tile([P, GW, 2], BF16, name="pb1_%d" % g, tag="pb1")
             words = pb[:].rearrange("p c e -> p (c e)").bitcast(F32)
@@ -189,9 +196,6 @@ def tile_differentiableilp_pa_kernel(tc, initial_facts, rule_weights, out):
 
         def last_spread(jj):
             g = NG - 1
-            nc.vector.tensor_tensor(
-                out=m12[g][:, jj:jj + 1], in0=m1[g][:, jj:jj + 1], in1=m2[g][:, jj:jj + 1], op=MAX
-            )
             pool, tag = (ps_b1, "pb1") if jj == 0 else (ps_tr, "tr")
             pm = pool.tile([P, P], F32, name="pm%d" % jj, tag=tag)
             nc.tensor.transpose(out=pm[:], in_=m12[g][:, jj:jj + 1].to_broadcast([P, P]), identity=ident_f[:])
@@ -322,9 +326,9 @@ def tile_differentiableilp_pa_kernel(tc, initial_facts, rule_weights, out):
         last_max_vector(g - 1, 0)
         last_max_vector(g - 1, 1)
         finish(g - 1)
-        best_rule(sums2[0], m2[g], 0)
+        best_of_steps(sums2[0], g, 0)
         pm0 = last_spread(0)
-        best_rule(sums2[1], m2[g], 1)
+        best_of_steps(sums2[1], g, 1)
         pm1 = last_spread(1)
         for h in range(2):
             last_direct(h, 0, pm0)

from contextlib import ExitStack

import concourse.mybir as mybir
from concourse.masks import make_identity

FP8X4 = mybir.dt.float8_e4m3fn_x4
BF16 = mybir.dt.bfloat16
F32 = mybir.dt.float32
U32 = mybir.dt.uint32
U8 = mybir.dt.uint8
MAX = mybir.AluOpType.max
MIN = mybir.AluOpType.min
MULT = mybir.AluOpType.mult
AX = mybir.AxisListType.X
EXP = mybir.ActivationFunctionType.Exp

P = 128
T = 4
R = 512
RB = R // P
C = 1536
GW = 256
NG = C // GW
BPG = GW // P

FLOPS = 2 * 2 * 512 * 512 * 1536

HEAD_REGROUPS = 4
NG_POOL = NG - 3
BF16_MAX = 3.3895313892515355e38


def tile_differentiableilp_pa_kernel(tc, initial_facts, rule_weights, out):
    nc = tc.nc
    facts_v = initial_facts.rearrange("(q t) c -> q t c", t=T)
    out_v = out.rearrange("(q t) c -> q t c", t=T)

    with ExitStack() as ctx:
        sb = ctx.enter_context(tc.tile_pool(name="sb", bufs=1))
        ps_s1 = ctx.enter_context(tc.psum_pool(name="ps_s1", bufs=2))
        ps_s2 = ctx.enter_context(tc.psum_pool(name="ps_s2", bufs=2))
        ps_b1 = ctx.enter_context(tc.psum_pool(name="ps_b1", bufs=1))
        ps_tr = ctx.enter_context(tc.psum_pool(name="ps_tr", bufs=1))
        ps_o = ctx.enter_context(tc.psum_pool(name="ps_o", bufs=2))
        ctx.enter_context(tc.manual_schedule())

        w_sb = [sb.tile([P, R], BF16, name="w_sb%d" % b) for b in range(RB)]
        f_sb = [sb.tile([P, T, GW], BF16, name="f_sb%d" % g) for g in range(NG)]
        ident_bf = sb.tile([P, P], BF16, name="ident_bf")
        ident_f = sb.tile([P, P], F32, name="ident_f")
        w_neg = [sb.tile([P, R], BF16, name="w_neg%d" % b) for b in range(RB)]
        junk = sb.tile([P, R], BF16, name="junk")
        warm = sb.tile([P, 2], F32, name="warm")
        nmax = sb.tile([P, RB], F32, name="nmax")
        ssum = sb.tile([P, RB], F32, name="ssum")
        rsum = sb.tile([P, RB], F32, name="rsum")
        e_sb = [sb.tile([P, R], F32, name="e_sb%d" % b) for b in range(RB)]
        a_bf = [sb.tile([P, R], BF16, name="a_bf%d" % b) for b in range(RB)]
        a_g = [sb.tile([P, P, T], BF16, name="a_g%d" % b, align_bytes=64) for b in range(RB)]
        a_q = sb.tile([P, R], U32, name="a_q", align_bytes=64)
        a_s = sb.tile([P, R], U8, name="a_s", align_bytes=64)
        f_g = [sb.tile([P, GW, T], BF16, name="f_g%d" % g, align_bytes=64) for g in range(NG)]
        f_q = [sb.tile([P, GW], U32, name="f_q%d" % g, align_bytes=64) for g in range(NG)]
        f_s = [sb.tile([P, GW], U8, name="f_s%d" % g, align_bytes=64) for g in range(NG)]
        g_g = [sb.tile([P, GW, T], BF16, name="g_g%d" % g, align_bytes=64) for g in range(NG)]
        g_q = [sb.tile([P, GW], U32, name="g_q%d" % g, align_bytes=64) for g in range(NG)]
        g_s = [sb.tile([P, GW], U8, name="g_s%d" % g, align_bytes=64) for g in range(NG)]
        m1 = [sb.tile([P, BPG], F32, name="m1_%d" % g) for g in range(NG)]
        m1p = [sb.tile([P, BPG, 2], BF16, name="m1p_%d" % g) for g in range(NG)]
        m2 = [sb.tile([P, BPG], F32, name="m2_%d" % g) for g in range(NG)]
        m12 = [sb.tile([P, BPG], F32, name="m12_%d" % g) for g in range(NG)]
        f_t = [sb.tile([P, BPG, R], BF16, name="f_t%d" % g) for g in range(NG - 1)]
        o_t = [sb.tile([P, BPG, R], F32, name="o_t%d" % g) for g in range(NG - 1)]
        o_sb = [sb.tile([P, T, GW], F32, name="o_sb%d" % g) for g in range(NG)]

        for b in range(RB):
            (nc.sync if b % 2 == 0 else nc.scalar).dma_start(out=w_sb[b][:], in_=rule_weights[b * P:(b + 1) * P, :])
        for g in range(NG):
            nc.sync.dma_start(out=f_sb[g][:], in_=facts_v[:, :, g * GW:(g + 1) * GW])

        nc.vector.memset(warm[:], 0.0)
        nc.scalar.activation(out=warm[:, 1:2], in_=warm[:, 0:1], func=EXP)
        make_identity(nc, ident_bf[:])
        make_identity(nc, ident_f[:])

        def regroup(copy, g):
            copy(
                out=f_g[g][:].rearrange("p (c i) t -> p c t i", i=4),
                in_=f_sb[g][:].rearrange("p t (c i) -> p c t i", i=4),
            )

        def pairs_of(tile):
            return tile[:].rearrange("p j k -> p (j k)").bitcast(F32)

        def words_of(tile):
            return tile[:].rearrange("p r t -> p (r t)").bitcast(F32).rearrange("p (r u) -> p r u", u=2)

        def regroup_block(g, jj):
            cols = slice(jj * P, (jj + 1) * P)
            nc.vector.tensor_copy(
                out=f_g[g][:, cols, :].rearrange("p (c i) t -> p c t i", i=4),
                in_=f_sb[g][:, :, cols].rearrange("p t (c i) -> p c t i", i=4),
            )

        def quantise_block(g, jj):
            cols = slice(jj * P, (jj + 1) * P)
            quantise(f_g[g][:, cols, :], f_q[g][:, cols], f_s[g][:, cols])

        def quantise(src, q, s):
            nc.vector.quantize_mx(out=q.bitcast(FP8X4), scales=s, in_=src.rearrange("p c t -> p (c t)"))

        def one_pass(pool, q, s, jj):
            acc = pool.tile([P, R], F32, name="acc", tag="acc")
            nc.tensor.matmul_mx(
                out=acc[:],
                lhsT=q[:, jj * P:(jj + 1) * P].bitcast(FP8X4),
                lhsT_scale=s[:, jj * P:(jj + 1) * P],
                rhs=a_q[:].bitcast(FP8X4),
                rhs_scale=a_s[:],
                start=True,
                stop=True,
            )
            return acc

        def best_rule(acc, m, jj):
            nc.vector.tensor_reduce(out=m[:, jj:jj + 1], in_=acc[:], axis=AX, op=MAX)

        def best_of_steps(acc, g, jj):
            nc.vector.tensor_scalar(
                out=junk[:], in0=acc[:], scalar1=1.0, scalar2=m1[g][:, jj:jj + 1], op0=MULT, op1=MAX,
                accum_out=m12[g][:, jj:jj + 1],
            )

        def spread1(g):
            pb = ps_b1.tile([P, GW, 2], BF16, name="pb1_%d" % g, tag="pb1")
            words = pb[:].rearrange("p c e -> p (c e)").bitcast(F32)
            pairs = m1p[g][:].rearrange("p j e -> p (j e)").bitcast(F32)
            for jj in range(BPG):
                nc.tensor.transpose(
                    out=words[:, jj * P:(jj + 1) * P], in_=pairs[:, jj:jj + 1].to_broadcast([P, P]), identity=ident_f[:]
                )
            return pb

        def facts1(g, pb):
            nc.vector.tensor_tensor(
                out=g_g[g][:].rearrange("p c (u e) -> p c u e", e=2),
                in0=f_g[g][:].rearrange("p c (u e) -> p c u e", e=2),
                in1=pb[:].unsqueeze(2).to_broadcast([P, GW, 2, 2]),
                op=MAX,
            )

        def flip_facts(g):
            pf = ps_tr.tile([P, BPG, R], BF16, name="pf%d" % g, tag="tr")
            for jj in range(BPG):
                for t in range(T):
                    nc.tensor.transpose(
                        out=pf[:, jj, t * P:(t + 1) * P], in_=f_sb[g][:, t, jj * P:(jj + 1) * P], identity=ident_bf[:]
                    )
            nc.scalar.copy(out=pairs_of(f_t[g]), in_=pairs_of(pf))

        def last_max_pool(g):
            for jj in range(BPG):
                nc.gpsimd.tensor_scalar(
                    out=m12[g][:, jj:jj + 1], in0=m2[g][:, jj:jj + 1], scalar1=m1[g][:, jj:jj + 1],
                    scalar2=None, op0=MAX,
                )
            for jj in range(BPG):
                nc.gpsimd.tensor_scalar(
                    out=o_t[g][:, jj, :], in0=f_t[g][:, jj, :], scalar1=BF16_MAX,
                    scalar2=m12[g][:, jj:jj + 1], op0=MIN, op1=MAX,
                )

        def last_max_vector(g, jj):
            nc.vector.tensor_scalar(
                out=o_t[g][:, jj, :], in0=f_t[g][:, jj, :], scalar1=m1[g][:, jj:jj + 1],
                scalar2=m2[g][:, jj:jj + 1], op0=MAX, op1=MAX,
            )

        def finish(g):
            for h in range(2):
                po = ps_o.tile([P, 2, GW], F32, name="po%d_%d" % (g, h), tag="po")
                for t in range(2):
                    for jj in range(BPG):
                        nc.tensor.transpose(
                            out=po[:, t, jj * P:(jj + 1) * P],
                            in_=o_t[g][:, jj, (2 * h + t) * P:(2 * h + t + 1) * P],
                            identity=ident_f[:],
                        )
                nc.scalar.copy(out=o_sb[g][:, 2 * h:2 * h + 2, :], in_=po[:])
                store_half(g, h)

        def store_half(g, h):
            nc.sync.dma_start(
                out=out_v[:, 2 * h:2 * h + 2, g * GW:(g + 1) * GW], in_=o_sb[g][:, 2 * h:2 * h + 2, :]
            )

        def last_spread(jj):
            g = NG - 1
            pool, tag = (ps_b1, "pb1") if jj == 0 else (ps_tr, "tr")
            pm = pool.tile([P, P], F32, name="pm%d" % jj, tag=tag)
            nc.tensor.transpose(out=pm[:], in_=m12[g][:, jj:jj + 1].to_broadcast([P, P]), identity=ident_f[:])
            return pm

        def last_direct(h, jj, pm):
            g = NG - 1
            nc.vector.tensor_tensor(
                out=o_sb[g][:, 2 * h:2 * h + 2, jj * P:(jj + 1) * P],
                in0=f_sb[g][:, 2 * h:2 * h + 2, jj * P:(jj + 1) * P],
                in1=pm[:].unsqueeze(1).to_broadcast([P, 2, P]), op=MAX,
            )

        pas = {}

        def row_max_exp(b):
            nc.vector.tensor_scalar(
                out=w_neg[b][:], in0=w_sb[b][:], scalar1=-1.0, scalar2=None, op0=MULT, op1=MIN,
                accum_out=nmax[:, b:b + 1],
            )
            nc.scalar.activation(
                out=e_sb[b][:], in_=w_sb[b][:], func=EXP, bias=nmax[:, b:b + 1], scale=1.0,
                accum_out=ssum[:, b:b + 1],
            )

        def inverse_sum(b):
            nc.vector.reciprocal(out=rsum[:, b:b + 1], in_=ssum[:, b:b + 1])

        def normalise(b):
            nc.vector.tensor_scalar(
                out=a_bf[b][:], in0=e_sb[b][:], scalar1=rsum[:, b:b + 1], scalar2=None, op0=MULT
            )
            words = a_bf[b][:].bitcast(F32)
            pas[b] = (ps_s1 if b < 2 else ps_s2).tile([P, 2, P], F32, name="pa%d" % b, tag="acc")
            for u in range(2):
                nc.tensor.transpose(out=pas[b][:, u, :], in_=words[:, u::2], identity=ident_f[:])

        def warm_up(b):
            idle = ps_o.tile([P, R], F32, name="idle", tag="po")
            nc.tensor.matmul(out=idle[:], lhsT=ident_bf[:], rhs=w_sb[b][:], start=True, stop=True)

        def lay_words(copy, b):
            copy(out=words_of(a_g[b]), in_=pas[b][:].rearrange("q u r -> q r u"))

        def quantise_rules(b):
            quantise(a_g[b][:], a_q[:, b * P:(b + 1) * P], a_s[:, b * P:(b + 1) * P])

        sums1 = [None, None]
        row_max_exp(0)
        row_max_exp(1)
        row_max_exp(2)
        row_max_exp(3)
        warm_up(0)
        warm_up(1)
        warm_up(2)
        inverse_sum(0)
        normalise(0)
        inverse_sum(1)
        normalise(1)
        warm_up(3)
        inverse_sum(2)
        regroup_block(0, 0)
        normalise(2)
        warm_up(0)
        inverse_sum(3)
        normalise(3)
        lay_words(nc.scalar.copy, 0)
        lay_words(nc.scalar.copy, 1)
        lay_words(nc.scalar.copy, 2)
        quantise_block(0, 0)
        warm_up(1)
        quantise_rules(0)
        regroup_block(0, 1)
        quantise_rules(1)
        lay_words(nc.vector.tensor_copy, 3)
        quantise_rules(2)
        quantise_rules(3)
        regroup(nc.scalar.copy, 1)
        regroup(nc.scalar.copy, 2)
        regroup(nc.scalar.copy, 3)
        sums1[0] = one_pass(ps_s1, f_q[0], f_s[0], 0)
        quantise_block(0, 1)
        sums1[1] = one_pass(ps_s1, f_q[0], f_s[0], 1)
        quantise(f_g[1][:], f_q[1][:], f_s[1][:])
        sums2 = [None, None]
        spread = {}

        for i in range(NG):
            for jj in range(BPG):
                if i < NG:
                    best_rule(sums1[jj], m1[i], jj)
                if i + 1 < NG:
                    sums1[jj] = one_pass(ps_s1, f_q[i + 1], f_s[i + 1], jj)
            if i < NG - 1:
                flip_facts(i)
            if i + HEAD_REGROUPS < NG:
                regroup(nc.scalar.copy, i + HEAD_REGROUPS)
            if 0 <= i - 3 < NG_POOL:
                finish(i - 3)
            if i >= 1:
                facts1(i - 1, spread[i - 1])
            if i < NG:
                nc.gpsimd.tensor_copy(out=m1p[i][:], in_=m1[i][:].unsqueeze(2).to_broadcast([P, BPG, 2]))
                spread[i] = spread1(i)
            for jj in range(BPG):
                if i >= 2:
                    best_rule(sums2[jj], m2[i - 2], jj)
                if i >= 1:
                    if jj == 0:
                        quantise(g_g[i - 1][:], g_q[i - 1][:], g_s[i - 1][:])
                    sums2[jj] = one_pass(ps_s2, g_q[i - 1], g_s[i - 1], jj)
            if i + 2 < NG:
                quantise(f_g[i + 2][:], f_q[i + 2][:], f_s[i + 2][:])
            if 0 <= i - 2 < NG_POOL:
                last_max_pool(i - 2)
            elif i - 2 >= NG_POOL:
                for jj in range(BPG):
                    last_max_vector(i - 2, jj)
                finish(i - 2)

        g = NG - 1
        facts1(g, spread[g])
        best_rule(sums2[0], m2[g - 1], 0)
        quantise(g_g[g][:], g_q[g][:], g_s[g][:])
        sums2[0] = one_pass(ps_s2, g_q[g], g_s[g], 0)
        best_rule(sums2[1], m2[g - 1], 1)
        sums2[1] = one_pass(ps_s2, g_q[g], g_s[g], 1)
        last_max_vector(g - 1, 0)
        last_max_vector(g - 1, 1)
        finish(g - 1)
        best_of_steps(sums2[0], g, 0)
        pm0 = last_spread(0)
        best_of_steps(sums2[1], g, 1)
        pm1 = last_spread(1)
        for h in range(2):
            last_direct(h, 0, pm0)
            last_direct(h, 1, pm1)
            store_half(g, h)
